import numpy as np
import ml_dtypes


def mxq(x, axis, fmt="e4m3"):
    dtype, down = {"e4m3": (ml_dtypes.float8_e4m3fn, 7), "e5m2": (ml_dtypes.float8_e5m2, 14)}[fmt]
    v = np.moveaxis(np.asarray(x, np.float32).astype(ml_dtypes.bfloat16).astype(np.float64), axis, -1)
    blocks = v.reshape(v.shape[:-1] + (-1, 32))
    amax = np.abs(blocks).max(-1, keepdims=True)
    byte = np.maximum(np.where(amax > 0, np.frexp(amax)[1] - 1 + 127, 0) - down, 1)
    scale = np.exp2(byte - 127.0)
    codes = (blocks / scale).astype(np.float32).astype(dtype).astype(np.float64)
    return np.moveaxis((codes * scale).reshape(v.shape), -1, axis)


WIDE = False


def mx_kscale(k):
    if not WIDE:
        return np.ones(k)
    levels = np.array([10, -10, 5, -5, 0])
    a = np.random.permutation(np.resize(levels, k // 512 * 4)).reshape(k // 512, 4)
    idx = np.arange(k)
    return np.exp2(a[idx // 512, idx % 128 // 32])


BF16 = ml_dtypes.bfloat16


def bf(x):
    return np.asarray(x, np.float32).astype(BF16)


def f64(x):
    return np.asarray(x).astype(np.float64)


B, T, E, H = 2, 512, 1024, 8
HD = E // H
S2 = 2 * T - 1


def rel_shift(m):
    b, h, t, p = m.shape
    mp = np.pad(m, ((0, 0), (0, 0), (0, 0), (1, 0)))
    mp = mp.reshape(b, h, p + 1, t)[:, :, 1:, :]
    return mp.reshape(b, h, t, p)[..., : p // 2 + 1]


def setup_inputs():
    s = mx_kscale(E)
    return {"q_u": bf(np.random.standard_normal((B, T, H, HD)) * 1.4),
            "k": bf(np.random.standard_normal((B, T, H, HD))),
            "matrix_bd": bf(np.random.standard_normal((B, H, T, S2)) * 1.4 * np.sqrt(HD)),
            "x": bf(np.random.standard_normal((B, T, E)) * s),
            "Wv": bf(np.random.standard_normal((E, E)) / np.sqrt(E) / s[None, :]),
            "bv": bf(np.random.standard_normal(E) * 0.3)}


def reference(q_u, k, matrix_bd, x, Wv, bv):
    v = (mxq(f64(x), 2, "e4m3") @ mxq(f64(Wv), 1, "e4m3").T) + f64(bv)
    v = v.reshape(B, T, H, HD).transpose(0, 2, 1, 3)
    matrix_ac = f64(q_u).transpose(0, 2, 1, 3) @ f64(k).transpose(0, 2, 3, 1)
    score = (matrix_ac + rel_shift(f64(matrix_bd))) * (1.0 / np.sqrt(HD))
    e = np.exp(score - score.max(-1, keepdims=True))
    o = (mxq(e, 3, "e4m3") @ mxq(v, 2, "e4m3")) / e.sum(-1, keepdims=True)
    return o.transpose(0, 2, 1, 3).reshape(B, T, E)

@@ -1,0 +1,361 @@
+import math
+from contextlib import ExitStack
+
+import concourse.mybir as mybir
+from concourse.masks import make_identity
+
+F32 = mybir.dt.float32
+BF16 = mybir.dt.bfloat16
+U32 = mybir.dt.uint32
+U8 = mybir.dt.uint8
+FP8X4 = mybir.dt.float8_e4m3fn_x4
+ALU = mybir.AluOpType
+ACT = mybir.ActivationFunctionType
+
+P = 128
+B = 2
+T = 512
+E = 1024
+H = 8
+HD = 128
+REL = 2 * T - 1
+TT = T // P
+PACK = 4
+K_PASS = P * PACK
+E_PASSES = E // K_PASS
+SCALE = 1.0 / math.sqrt(HD)
+GROUP = 4
+N_HEADS = B * H
+N_HALVES = N_HEADS * 2
+N_TILES = N_HEADS * TT
+
+QK_LEAD = 3
+E_T_LAG = 4
+X_LAG = 2
+V_LAG = 8
+NORMALISE_LAG = V_LAG + TT + 1
+
+FLOPS = 2 * B * T * E * E + 2 * 2 * B * H * T * T * HD
+BYTES = 2 * (3 * B * T * E + E * E + E + B * H * T * T) + 4 * B * T * E
+
+
+def unit(slot, period, count):
+    if slot % period == 0 and 0 <= slot // period < count:
+        return slot // period
+    return None
+
+
+def tile_attentionforonnx_pa_kernel(tc, q_u, k, matrix_bd, x, Wv, bv, out):
+    nc = tc.nc
+    with ExitStack() as ctx:
+        const = ctx.enter_context(tc.tile_pool(name="const", bufs=1))
+        raw = ctx.enter_context(tc.tile_pool(name="raw", bufs=2))
+        work = ctx.enter_context(tc.tile_pool(name="work", bufs=3))
+        psum_t = ctx.enter_context(tc.psum_pool(name="psum_t", bufs=2))
+        psum_ac = ctx.enter_context(tc.psum_pool(name="psum_ac", bufs=2))
+        psum_e = ctx.enter_context(tc.psum_pool(name="psum_e", bufs=2))
+        psum_mx = ctx.enter_context(tc.psum_pool(name="psum_mx", bufs=2))
+        ctx.enter_context(tc.manual_schedule())
+
+        k_raw, q_raw, x_raw, bd_sb, qk_t, ac_ps = {}, {}, {}, {}, {}, {}
+        score, neg_max, e_sb, row_sum, inv_sum = {}, {}, {}, {}, {}
+        e_ps, e_grouped, e_codes, e_scales = {}, {}, {}, {}
+        x_grouped, x_codes, x_scales, w_grouped = {}, {}, {}, {}
+        v_ps, v_grouped, v_codes, v_scales, o_ps, o_sb = {}, {}, {}, {}, {}, {}
+
+        warm = const.tile([P, 1], F32, name="warm")
+        nc.vector.memset(warm[:], 0.0)
+        nc.scalar.activation(out=warm[:], in_=warm[:], func=ACT.Exp)
+        ident_bf = const.tile([P, P], BF16, name="ident_bf")
+        make_identity(nc, ident_bf[:])
+        ident_f32 = const.tile([P, P], F32, name="ident_f32")
+        make_identity(nc, ident_f32[:])
+        bias_bc = const.tile([P, E], BF16, name="bias_bc")
+        nc.gpsimd.dma_start(out=bias_bc[:], in_=bv.partition_broadcast(P))
+        w_raw = const.tile([P, H, E], BF16, name="w_raw")
+        w_codes = const.tile([P, H, E_PASSES, P], U32, name="w_codes", align_bytes=64)
+        w_scales = const.tile([P, H, E_PASSES, P], U8, name="w_scales", align_bytes=64)
+
+        bd_flat = matrix_bd.rearrange("b h t r -> b h (t r)")
+
+        def request_group(g):
+            if g >= N_HEADS // GROUP:
+                return
+            b = g * GROUP // H
+            cols = slice((g * GROUP % H) * HD, (g * GROUP % H + GROUP) * HD)
+            k_raw[g] = raw.tile([P, TT, GROUP * HD], BF16, name="k_raw", bufs=N_HEADS // GROUP)
+            q_raw[g] = raw.tile([P, TT, GROUP * HD], BF16, name="q_raw", bufs=N_HEADS // GROUP)
+            nc.sync.dma_start(
+                out=k_raw[g][:], in_=k[b].rearrange("(a p) h d -> p a (h d)", p=P)[:, :, cols]
+            )
+            nc.sync.dma_start(
+                out=q_raw[g][:], in_=q_u[b].rearrange("(a p) h d -> p a (h d)", p=P)[:, :, cols]
+            )
+
+        def request_x(b):
+            if b >= B:
+                return
+            x_raw[b] = raw.tile([P, PACK, E], BF16, name="x_raw")
+            nc.sync.dma_start(
+                out=x_raw[b][:].rearrange("p (u e) f -> p u (e f)", u=2),
+                in_=x[b].rearrange("(u p e) f -> p u (e f)", u=2, p=P),
+            )
+
+        def request_head(i):
+            if i >= N_HEADS:
+                return
+            window = bd_flat[i // H, i % H, T - 1 : T - 1 + T * (REL - 1)]
+            window = window.rearrange("(a p c) -> p a c", a=TT, p=P)
+            bd_sb[i] = work.tile([P, TT, T], BF16, name="bd_sb", bufs=4)
+            nc.sync.dma_start(out=bd_sb[i][:], in_=window[:, :, 0:T])
+            if i < H:
+                nc.sync.dma_start(out=w_raw[:, i, :], in_=Wv[i * HD : (i + 1) * HD, :])
+
+        def regroup_rows(rows, grouped):
+            words = rows.bitcast(F32)
+            t_ps = psum_t.tile([P, 2 * E_PASSES, P], F32, name="t_ps", tag="tp")
+            for g in range(2 * E_PASSES):
+                nc.tensor.transpose(t_ps[:, g, :], words[:, g * P : (g + 1) * P], ident_f32[:])
+            nc.scalar.copy(out=grouped, in_=t_ps[:].rearrange("p (c u) n -> p c n u", u=2))
+
+        def regroup_x(b, r):
+            if r == 0:
+                x_grouped[b] = work.tile(
+                    [P, PACK, E_PASSES, P, 2], F32, name="x_grouped", bufs=2, align_bytes=64
+                )
+            regroup_rows(x_raw[b][:, r, :], x_grouped[b][:, r])
+
+        def quantise_x(b):
+            x_codes[b] = work.tile([P, PACK, E_PASSES, P], U32, name="x_codes", bufs=2, align_bytes=64)
+            x_scales[b] = work.tile([P, PACK, E_PASSES, P], U8, name="x_scales", bufs=2, align_bytes=64)
+            nc.vector.quantize_mx(
+                out=x_codes[b][:].rearrange("p r c n -> p (r c n)").bitcast(FP8X4),
+                scales=x_scales[b][:].rearrange("p r c n -> p (r c n)"),
+                in_=x_grouped[b][:].rearrange("p r c n u -> p (r c n u)").bitcast(BF16),
+            )
+
+        def regroup_w(h):
+            w_grouped[h] = work.tile([P, E_PASSES, P, 2], F32, name="w_grouped", bufs=2, align_bytes=64)
+            regroup_rows(w_raw[:, h, :], w_grouped[h][:])
+
+        def quantise_w(h):
+            nc.vector.quantize_mx(
+                out=w_codes[:, h].rearrange("p c n -> p (c n)").bitcast(FP8X4),
+                scales=w_scales[:, h].rearrange("p c n -> p (c n)"),
+                in_=w_grouped[h][:].rearrange("p c n u -> p (c n u)").bitcast(BF16),
+            )
+
+        def project_values(i):
+            b, h = i // H, i % H
+            v_ps[i] = psum_mx.tile([P, PACK, HD], F32, name="v_ps", tag="mx")
+            for j in range(PACK):
+                for c in range(E_PASSES):
+                    nc.tensor.matmul_mx(
+                        out=v_ps[i][:, j, :],
+                        lhsT=x_codes[b][:, j, c, :].bitcast(FP8X4),
+                        lhsT_scale=x_scales[b][:, j, c, :],
+                        rhs=w_codes[:, h, c, :].bitcast(FP8X4),
+                        rhs_scale=w_scales[:, h, c, :],
+                        start=(c == 0),
+                        stop=(c == E_PASSES - 1),
+                    )
+
+        def add_bias(i):
+            h = i % H
+            v_grouped[i] = work.tile([P, HD, PACK], BF16, name="v_grouped", align_bytes=64)
+            bias = bias_bc[:, h * HD : (h + 1) * HD].unsqueeze(2).to_broadcast([P, HD, PACK])
+            nc.vector.tensor_tensor(
+                out=v_grouped[i][:], in0=v_ps[i][:].rearrange("p j d -> p d j"), in1=bias, op=ALU.add
+            )
+
+        def quantise_v(i):
+            v_codes[i] = work.tile([P, HD], U32, name="v_codes", align_bytes=64)
+            v_scales[i] = work.tile([P, HD], U8, name="v_scales", align_bytes=64)
+            nc.vector.quantize_mx(
+                out=v_codes[i][:].bitcast(FP8X4),
+                scales=v_scales[i][:],
+                in_=v_grouped[i][:].rearrange("p d j -> p (d j)"),
+            )
+
+        def transpose_qk(i):
+            g = i // GROUP
+            cols = slice((i % GROUP) * HD, (i % GROUP + 1) * HD)
+            qk_ps = psum_t.tile([P, 2, T], BF16, name="qk_ps", tag="tp")
+            for a in range(TT):
+                nc.tensor.transpose(qk_ps[:, 0, a * P : (a + 1) * P], q_raw[g][:, a, cols], ident_bf[:])
+            for a in range(TT):
+                nc.tensor.transpose(qk_ps[:, 1, a * P : (a + 1) * P], k_raw[g][:, a, cols], ident_bf[:])
+            qk_t[i] = work.tile([P, 2, T], BF16, name="qk_t")
+            nc.scalar.copy(out=qk_t[i][:], in_=qk_ps[:])
+
+        def content_scores(n):
+            i, a = n // TT, n % TT
+            ac_ps[n] = psum_ac.tile([P, T], F32, name="ac_ps")
+            nc.tensor.matmul(
+                ac_ps[n][:], lhsT=qk_t[i][:, 0, a * P : (a + 1) * P], rhs=qk_t[i][:, 1, :],
+                start=True, stop=True,
+            )
+
+        def add_shifted(n):
+            i, a = n // TT, n % TT
+            if a == 0:
+                score[i] = work.tile([P, TT, T], F32, name="score")
+                neg_max[i] = work.tile([P, TT], F32, name="neg_max")
+            nc.vector.tensor_tensor(
+                out=score[i][:, a, :], in0=ac_ps[n][:], in1=bd_sb[i][:, a, :], op=ALU.add
+            )
+
+        def scale_and_min(n):
+            i, a = n // TT, n % TT
+            nc.vector.tensor_scalar(
+                out=score[i][:, a, :], in0=score[i][:, a, :], scalar1=-SCALE, scalar2=None,
+                op0=ALU.mult, op1=ALU.min, accum_out=neg_max[i][:, a : a + 1],
+            )
+
+        def exponentials(n):
+            i, a = n // TT, n % TT
+            if a == 0:
+                e_sb[i] = work.tile([P, TT, T], BF16, name="e_sb")
+                row_sum[i] = work.tile([P, TT], F32, name="row_sum", bufs=4)
+            nc.scalar.activation(
+                out=e_sb[i][:, a, :], in_=score[i][:, a, :], func=ACT.Exp,
+                bias=neg_max[i][:, a : a + 1], scale=-1.0, accum_out=row_sum[i][:, a : a + 1],
+            )
+
+        def transpose_e(n):
+            i, a, m = n // TT, n % TT, n // 2
+            if n % 2 == 0:
+                e_ps[m] = psum_e.tile([P, 2, 2 * P], F32, name="e_ps")
+            words = e_sb[i][:].bitcast(F32)
+            for u in range(2):
+                nc.tensor.transpose(
+                    e_ps[m][:, u, (n % 2) * P : (n % 2 + 1) * P],
+                    words[:, a, u * P : (u + 1) * P],
+                    ident_f32[:],
+                )
+
+        def regroup_e(m):
+            i = m // 2
+            if m % 2 == 0:
+                e_grouped[i] = work.tile([P, T * PACK], BF16, name="e_grouped", align_bytes=64)
+            words = e_grouped[i][:].bitcast(F32).rearrange("p (t u) -> p t u", u=2)
+            nc.scalar.copy(
+                out=words[:, (m % 2) * 2 * P : (m % 2 + 1) * 2 * P, :],
+                in_=e_ps[m][:].rearrange("p u t -> p t u"),
+            )
+
+        def quantise_e(m):
+            i = m // 2
+            if m % 2 == 0:
+                e_codes[i] = work.tile([P, T], U32, name="e_codes", bufs=5, align_bytes=64)
+                e_scales[i] = work.tile([P, T], U8, name="e_scales", bufs=5, align_bytes=64)
+            queries = slice((m % 2) * 2 * P, (m % 2 + 1) * 2 * P)
+            nc.vector.quantize_mx(
+                out=e_codes[i][:, queries].bitcast(FP8X4),
+                scales=e_scales[i][:, queries],
+                in_=e_grouped[i][:, (m % 2) * 2 * P * PACK : (m % 2 + 1) * 2 * P * PACK],
+            )
+
+        def invert_sums(i):
+            inv_sum[i] = work.tile([P, TT], F32, name="inv_sum", bufs=4)
+            nc.vector.reciprocal(inv_sum[i][:], row_sum[i][:])
+
+        def attend(i):
+            o_ps[i] = psum_mx.tile([P, TT, HD], F32, name="o_ps", tag="mx")
+            for a in range(TT):
+                nc.tensor.matmul_mx(
+                    out=o_ps[i][:, a, :],
+                    lhsT=e_codes[i][:, a * P : (a + 1) * P].bitcast(FP8X4),
+                    lhsT_scale=e_scales[i][:, a * P : (a + 1) * P],
+                    rhs=v_codes[i][:].bitcast(FP8X4),
+                    rhs_scale=v_scales[i][:],
+                    start=True,
+                    stop=True,
+                )
+
+        def normalise(m):
+            i = m // 2
+            if m % 2 == 0:
+                o_sb[i] = work.tile([P, TT, HD], F32, name="o_sb")
+            for a in range(2 * (m % 2), 2 * (m % 2) + 2):
+                nc.scalar.activation(
+                    out=o_sb[i][:, a, :], in_=o_ps[i][:, a, :], func=ACT.Copy,
+                    scale=inv_sum[i][:, a : a + 1],
+                )
+            if m % 2 == 1:
+                b, h = i // H, i % H
+                nc.sync.dma_start(
+                    out=out[b].rearrange("(a p) e -> p a e", p=P)[:, :, h * HD : (h + 1) * HD],
+                    in_=o_sb[i][:],
+                )
+
+        request_group(0)
+        request_head(0)
+        request_x(0)
+        request_head(1)
+        for n in range(-QK_LEAD, N_TILES + NORMALISE_LAG - 1):
+            i = unit(n, TT, N_HEADS)
+            if i is not None:
+                request_head(i + 2)
+                if i % GROUP == 0:
+                    request_group(i // GROUP + 1)
+                if (i + GROUP) % H == 0:
+                    request_x((i + GROUP) // H)
+
+            t = unit(n + 1, 1, N_TILES)
+            if t is not None:
+                content_scores(t)
+            t = unit(n, 1, N_TILES)
+            if t is not None:
+                add_shifted(t)
+            t = unit(n - 1, 1, N_TILES)
+            if t is not None:
+                scale_and_min(t)
+            t = unit(n - 2, 1, N_TILES)
+            if t is not None:
+                exponentials(t)
+            t = unit(n - E_T_LAG, 1, N_TILES)
+            if t is not None:
+                transpose_e(t)
+            m = unit(n - E_T_LAG - 2, 2, N_HALVES)
+            if m is not None:
+                regroup_e(m)
+            m = unit(n - E_T_LAG - 3, 2, N_HALVES)
+            if m is not None:
+                quantise_e(m)
+
+            i = unit(n + QK_LEAD, TT, N_HEADS)
+            if i is not None:
+                transpose_qk(i)
+            for b in range(B):
+                if 0 <= n - X_LAG - b * H * TT < PACK:
+                    regroup_x(b, n - X_LAG - b * H * TT)
+            i = unit(n - V_LAG + 2, TT, H)
+            if i is not None:
+                regroup_w(i)
+
+            i = unit(n - V_LAG, TT, N_HEADS)
+            if i is not None:
+                invert_sums(i)
+            b = unit(n - V_LAG + 1, H * TT, B)
+            if b is not None:
+                quantise_x(b)
+            i = unit(n - V_LAG + 1, TT, H)
+            if i is not None:
+                quantise_w(i)
+            i = unit(n - V_LAG - 1, TT, N_HEADS)
+            if i is not None:
+                add_bias(i)
+            i = unit(n - V_LAG - 2, TT, N_HEADS)
+            if i is not None:
+                quantise_v(i)
+
+            i = unit(n - V_LAG - TT, TT, N_HEADS)
+            if i is not None:
+                attend(i)
+            i = unit(n - V_LAG, TT, N_HEADS)
+            if i is not None:
+                project_values(i)
+            m = unit(n - NORMALISE_LAG, 2, N_HALVES)
+            if m is not None:
+                normalise(m)

@@ -24,13 +24,15 @@ PACK = 4
 K_PASS = P * PACK
 E_PASSES = E // K_PASS
 SCALE = 1.0 / math.sqrt(HD)
-GROUP = 4
+GROUP = 2
 N_HEADS = B * H
 N_HALVES = N_HEADS * 2
 N_TILES = N_HEADS * TT
 
 QK_LEAD = 3
-E_T_LAG = 4
+EXP_LAG = 3
+E_T_LAG = 5
+X_AHEAD = 4
 X_LAG = 2
 V_LAG = 8
 NORMALISE_LAG = V_LAG + TT + 1
@@ -58,7 +60,7 @@ def tile_attentionforonnx_pa_kernel(tc, q_u, k, matrix_bd, x, Wv, bv, out):
         ctx.enter_context(tc.manual_schedule())
 
         k_raw, q_raw, x_raw, bd_sb, qk_t, ac_ps = {}, {}, {}, {}, {}, {}
-        score, neg_max, e_sb, row_sum, inv_sum = {}, {}, {}, {}, {}
+        score, row_max, neg_max, e_sb, row_sum, inv_sum = {}, {}, {}, {}, {}, {}
         e_ps, e_grouped, e_codes, e_scales = {}, {}, {}, {}
         x_grouped, x_codes, x_scales, w_grouped = {}, {}, {}, {}
         v_ps, v_grouped, v_codes, v_scales, o_ps, o_sb = {}, {}, {}, {}, {}, {}
@@ -200,16 +202,21 @@ def tile_attentionforonnx_pa_kernel(tc, q_u, k, matrix_bd, x, Wv, bv, out):
             i, a = n // TT, n % TT
             if a == 0:
                 score[i] = work.tile([P, TT, T], F32, name="score")
+                row_max[i] = work.tile([P, TT], F32, name="row_max")
                 neg_max[i] = work.tile([P, TT], F32, name="neg_max")
             nc.vector.tensor_tensor(
                 out=score[i][:, a, :], in0=ac_ps[n][:], in1=bd_sb[i][:, a, :], op=ALU.add
             )
 
-        def scale_and_min(n):
+        def maximum(n):
             i, a = n // TT, n % TT
-            nc.vector.tensor_scalar(
-                out=score[i][:, a, :], in0=score[i][:, a, :], scalar1=-SCALE, scalar2=None,
-                op0=ALU.mult, op1=ALU.min, accum_out=neg_max[i][:, a : a + 1],
+            nc.vector.tensor_reduce(
+                out=row_max[i][:, a : a + 1], in_=score[i][:, a, :], axis=mybir.AxisListType.X,
+                op=ALU.max,
+            )
+            nc.gpsimd.tensor_scalar(
+                out=neg_max[i][:, a : a + 1], in0=row_max[i][:, a : a + 1], scalar1=-SCALE,
+                scalar2=0.0, op0=ALU.mult, op1=ALU.add,
             )
 
         def exponentials(n):
@@ -219,7 +226,7 @@ def tile_attentionforonnx_pa_kernel(tc, q_u, k, matrix_bd, x, Wv, bv, out):
                 row_sum[i] = work.tile([P, TT], F32, name="row_sum", bufs=4)
             nc.scalar.activation(
                 out=e_sb[i][:, a, :], in_=score[i][:, a, :], func=ACT.Exp,
-                bias=neg_max[i][:, a : a + 1], scale=-1.0, accum_out=row_sum[i][:, a : a + 1],
+                bias=neg_max[i][:, a : a + 1], scale=SCALE, accum_out=row_sum[i][:, a : a + 1],
             )
 
         def transpose_e(n):
@@ -293,14 +300,15 @@ def tile_attentionforonnx_pa_kernel(tc, q_u, k, matrix_bd, x, Wv, bv, out):
         request_head(0)
         request_x(0)
         request_head(1)
+        request_group(1)
         for n in range(-QK_LEAD, N_TILES + NORMALISE_LAG - 1):
             i = unit(n, TT, N_HEADS)
             if i is not None:
                 request_head(i + 2)
                 if i % GROUP == 0:
-                    request_group(i // GROUP + 1)
-                if (i + GROUP) % H == 0:
-                    request_x((i + GROUP) // H)
+                    request_group(i // GROUP + 2)
+                if (i + X_AHEAD) % H == 0:
+                    request_x((i + X_AHEAD) // H)
 
             t = unit(n + 1, 1, N_TILES)
             if t is not None:
@@ -310,8 +318,8 @@ def tile_attentionforonnx_pa_kernel(tc, q_u, k, matrix_bd, x, Wv, bv, out):
                 add_shifted(t)
             t = unit(n - 1, 1, N_TILES)
             if t is not None:
-                scale_and_min(t)
-            t = unit(n - 2, 1, N_TILES)
+                maximum(t)
+            t = unit(n - EXP_LAG, 1, N_TILES)
             if t is not None:
                 exponentials(t)
             t = unit(n - E_T_LAG, 1, N_TILES)

@@ -33,8 +33,9 @@ QK_LEAD = 3
 EXP_LAG = 3
 E_T_LAG = 5
 X_AHEAD = 4
-X_LAG = 2
-V_LAG = 8
+V_LAG = 9
+TENSOR_ADDS = 12
+TENSOR_ADD_EVERY = 5
 NORMALISE_LAG = V_LAG + TT + 1
 
 FLOPS = 2 * B * T * E * E + 2 * 2 * B * H * T * T * HD
@@ -47,20 +48,25 @@ def unit(slot, period, count):
     return None
 
 
+def added_on_tensor(n):
+    return n % TENSOR_ADD_EVERY == 0 and n // TENSOR_ADD_EVERY < TENSOR_ADDS
+
+
 def tile_attentionforonnx_pa_kernel(tc, q_u, k, matrix_bd, x, Wv, bv, out):
     nc = tc.nc
     with ExitStack() as ctx:
         const = ctx.enter_context(tc.tile_pool(name="const", bufs=1))
         raw = ctx.enter_context(tc.tile_pool(name="raw", bufs=2))
         work = ctx.enter_context(tc.tile_pool(name="work", bufs=3))
-        psum_t = ctx.enter_context(tc.psum_pool(name="psum_t", bufs=2))
+        psum_t = ctx.enter_context(tc.psum_pool(name="psum_t", bufs=1))
+        psum_sum = ctx.enter_context(tc.psum_pool(name="psum_sum", bufs=1))
         psum_ac = ctx.enter_context(tc.psum_pool(name="psum_ac", bufs=2))
         psum_e = ctx.enter_context(tc.psum_pool(name="psum_e", bufs=2))
         psum_mx = ctx.enter_context(tc.psum_pool(name="psum_mx", bufs=2))
         ctx.enter_context(tc.manual_schedule())
 
         k_raw, q_raw, x_raw, bd_sb, qk_t, ac_ps = {}, {}, {}, {}, {}, {}
-        score, row_max, neg_max, e_sb, row_sum, inv_sum = {}, {}, {}, {}, {}, {}
+        score, summed, row_max, neg_max, e_sb, row_sum, inv_sum = {}, {}, {}, {}, {}, {}, {}
         e_ps, e_grouped, e_codes, e_scales = {}, {}, {}, {}
         x_grouped, x_codes, x_scales, w_grouped = {}, {}, {}, {}
         v_ps, v_grouped, v_codes, v_scales, o_ps, o_sb = {}, {}, {}, {}, {}, {}
@@ -184,9 +190,9 @@ def tile_attentionforonnx_pa_kernel(tc, q_u, k, matrix_bd, x, Wv, bv, out):
             cols = slice((i % GROUP) * HD, (i % GROUP + 1) * HD)
             qk_ps = psum_t.tile([P, 2, T], BF16, name="qk_ps", tag="tp")
             for a in range(TT):
-                nc.tensor.transpose(qk_ps[:, 0, a * P : (a + 1) * P], q_raw[g][:, a, cols], ident_bf[:])
-            for a in range(TT):
                 nc.tensor.transpose(qk_ps[:, 1, a * P : (a + 1) * P], k_raw[g][:, a, cols], ident_bf[:])
+            for a in range(TT):
+                nc.tensor.transpose(qk_ps[:, 0, a * P : (a + 1) * P], q_raw[g][:, a, cols], ident_bf[:])
             qk_t[i] = work.tile([P, 2, T], BF16, name="qk_t")
             nc.scalar.copy(out=qk_t[i][:], in_=qk_ps[:])
 
@@ -204,14 +210,26 @@ def tile_attentionforonnx_pa_kernel(tc, q_u, k, matrix_bd, x, Wv, bv, out):
                 score[i] = work.tile([P, TT, T], F32, name="score")
                 row_max[i] = work.tile([P, TT], F32, name="row_max")
                 neg_max[i] = work.tile([P, TT], F32, name="neg_max")
-            nc.vector.tensor_tensor(
-                out=score[i][:, a, :], in0=ac_ps[n][:], in1=bd_sb[i][:, a, :], op=ALU.add
-            )
+            if added_on_tensor(n):
+                sum_ps = psum_sum.tile([P, T], F32, name="sum_ps")
+                nc.tensor.matmul(
+                    sum_ps[:], lhsT=qk_t[i][:, 0, a * P : (a + 1) * P], rhs=qk_t[i][:, 1, :],
+                    start=True, stop=False,
+                )
+                nc.tensor.matmul(
+                    sum_ps[:], lhsT=ident_bf[:], rhs=bd_sb[i][:, a, :], start=False, stop=True
+                )
+                summed[n] = sum_ps[:]
+            else:
+                summed[n] = score[i][:, a, :]
+                nc.vector.tensor_tensor(
+                    out=summed[n], in0=ac_ps[n][:], in1=bd_sb[i][:, a, :], op=ALU.add
+                )
 
         def maximum(n):
             i, a = n // TT, n % TT
             nc.vector.tensor_reduce(
-                out=row_max[i][:, a : a + 1], in_=score[i][:, a, :], axis=mybir.AxisListType.X,
+                out=row_max[i][:, a : a + 1], in_=summed[n], axis=mybir.AxisListType.X,
                 op=ALU.max,
             )
             nc.gpsimd.tensor_scalar(
@@ -225,7 +243,7 @@ def tile_attentionforonnx_pa_kernel(tc, q_u, k, matrix_bd, x, Wv, bv, out):
                 e_sb[i] = work.tile([P, TT, T], BF16, name="e_sb")
                 row_sum[i] = work.tile([P, TT], F32, name="row_sum", bufs=4)
             nc.scalar.activation(
-                out=e_sb[i][:, a, :], in_=score[i][:, a, :], func=ACT.Exp,
+                out=e_sb[i][:, a, :], in_=summed[n], func=ACT.Exp,
                 bias=neg_max[i][:, a : a + 1], scale=SCALE, accum_out=row_sum[i][:, a : a + 1],
             )
 
@@ -311,7 +329,7 @@ def tile_attentionforonnx_pa_kernel(tc, q_u, k, matrix_bd, x, Wv, bv, out):
                     request_x((i + X_AHEAD) // H)
 
             t = unit(n + 1, 1, N_TILES)
-            if t is not None:
+            if t is not None and not added_on_tensor(t):
                 content_scores(t)
             t = unit(n, 1, N_TILES)
             if t is not None:
@@ -336,9 +354,10 @@ def tile_attentionforonnx_pa_kernel(tc, q_u, k, matrix_bd, x, Wv, bv, out):
             if i is not None:
                 transpose_qk(i)
             for b in range(B):
-                if 0 <= n - X_LAG - b * H * TT < PACK:
-                    regroup_x(b, n - X_LAG - b * H * TT)
-            i = unit(n - V_LAG + 2, TT, H)
+                since = n - b * H * TT
+                if 0 <= since < 2 * TT and since % TT >= 2:
+                    regroup_x(b, 2 * (since // TT) + since % TT - 2)
+            i = unit(n - TT, TT, H)
             if i is not None:
                 regroup_w(i)
 

@@ -35,8 +35,8 @@ E_T_LAG = 5
 X_AHEAD = 4
 V_LAG = 9
 TENSOR_ADDS = 12
-TENSOR_ADD_EVERY = 5
-NORMALISE_LAG = V_LAG + TT + 1
+ATTEND_LAG = V_LAG + TT + 2
+NORMALISE_LAG = ATTEND_LAG + 1
 
 FLOPS = 2 * B * T * E * E + 2 * 2 * B * H * T * T * HD
 BYTES = 2 * (3 * B * T * E + E * E + E + B * H * T * T) + 4 * B * T * E
@@ -49,7 +49,7 @@ def unit(slot, period, count):
 
 
 def added_on_tensor(n):
-    return n % TENSOR_ADD_EVERY == 0 and n // TENSOR_ADD_EVERY < TENSOR_ADDS
+    return n % TT == 0 and n // TT < TENSOR_ADDS
 
 
 def tile_attentionforonnx_pa_kernel(tc, q_u, k, matrix_bd, x, Wv, bv, out):
@@ -153,10 +153,11 @@ def tile_attentionforonnx_pa_kernel(tc, q_u, k, matrix_bd, x, Wv, bv, out):
                 in_=w_grouped[h][:].rearrange("p c n u -> p (c n u)").bitcast(BF16),
             )
 
-        def project_values(i):
+        def project_values(i, part):
             b, h = i // H, i % H
-            v_ps[i] = psum_mx.tile([P, PACK, HD], F32, name="v_ps", tag="mx")
-            for j in range(PACK):
+            if part == 0:
+                v_ps[i] = psum_mx.tile([P, PACK, HD], F32, name="v_ps", tag="mx")
+            for j in range(2 * part, 2 * part + 2):
                 for c in range(E_PASSES):
                     nc.tensor.matmul_mx(
                         out=v_ps[i][:, j, :],
@@ -272,8 +273,8 @@ def tile_attentionforonnx_pa_kernel(tc, q_u, k, matrix_bd, x, Wv, bv, out):
         def quantise_e(m):
             i = m // 2
             if m % 2 == 0:
-                e_codes[i] = work.tile([P, T], U32, name="e_codes", bufs=5, align_bytes=64)
-                e_scales[i] = work.tile([P, T], U8, name="e_scales", bufs=5, align_bytes=64)
+                e_codes[i] = work.tile([P, T], U32, name="e_codes", bufs=6, align_bytes=64)
+                e_scales[i] = work.tile([P, T], U8, name="e_scales", bufs=6, align_bytes=64)
             queries = slice((m % 2) * 2 * P, (m % 2 + 1) * 2 * P)
             nc.vector.quantize_mx(
                 out=e_codes[i][:, queries].bitcast(FP8X4),
@@ -370,19 +371,20 @@ def tile_attentionforonnx_pa_kernel(tc, q_u, k, matrix_bd, x, Wv, bv, out):
             i = unit(n - V_LAG + 1, TT, H)
             if i is not None:
                 quantise_w(i)
-            i = unit(n - V_LAG - 1, TT, N_HEADS)
+            i = unit(n - V_LAG - 2, TT, N_HEADS)
             if i is not None:
                 add_bias(i)
-            i = unit(n - V_LAG - 2, TT, N_HEADS)
+            i = unit(n - V_LAG - 3, TT, N_HEADS)
             if i is not None:
                 quantise_v(i)
 
-            i = unit(n - V_LAG - TT, TT, N_HEADS)
+            i = unit(n - ATTEND_LAG, TT, N_HEADS)
             if i is not None:
                 attend(i)
-            i = unit(n - V_LAG, TT, N_HEADS)
-            if i is not None:
-                project_values(i)
+            for part in range(2):
+                i = unit(n - V_LAG - part, TT, N_HEADS)
+                if i is not None:
+                    project_values(i, part)
             m = unit(n - NORMALISE_LAG, 2, N_HALVES)
             if m is not None:
                 normalise(m)

@@ -29,14 +29,17 @@ N_HEADS = B * H
 N_HALVES = N_HEADS * 2
 N_TILES = N_HEADS * TT
 
-QK_LEAD = 3
-EXP_LAG = 3
-E_T_LAG = 5
-X_AHEAD = 4
-V_LAG = 9
+EXP_LAG = 4
+E_T_LAG = 6
+REGROUP_LAG = 9
+QUANT_LAG = 10
+QK_LAG = -3
+X_LAG = 2
+W_LAG = 7
+VALUE_LAG = 12
+ATTEND_LAG = 18
+
 TENSOR_ADDS = 12
-ATTEND_LAG = V_LAG + TT + 2
-NORMALISE_LAG = ATTEND_LAG + 1
 
 FLOPS = 2 * B * T * E * E + 2 * 2 * B * H * T * T * HD
 BYTES = 2 * (3 * B * T * E + E * E + E + B * H * T * T) + 4 * B * T * E
@@ -49,7 +52,7 @@ def unit(slot, period, count):
 
 
 def added_on_tensor(n):
-    return n % TT == 0 and n // TT < TENSOR_ADDS
+    return n % TT == 0 and 1 <= n // TT <= TENSOR_ADDS
 
 
 def tile_attentionforonnx_pa_kernel(tc, q_u, k, matrix_bd, x, Wv, bv, out):
@@ -65,10 +68,10 @@ def tile_attentionforonnx_pa_kernel(tc, q_u, k, matrix_bd, x, Wv, bv, out):
         psum_mx = ctx.enter_context(tc.psum_pool(name="psum_mx", bufs=2))
         ctx.enter_context(tc.manual_schedule())
 
-        k_raw, q_raw, x_raw, bd_sb, qk_t, ac_ps = {}, {}, {}, {}, {}, {}
+        k_raw, q_raw, x_raw, bd_sb, qk_ps, qk_t, ac_ps = {}, {}, {}, {}, {}, {}, {}
         score, summed, row_max, neg_max, e_sb, row_sum, inv_sum = {}, {}, {}, {}, {}, {}, {}
         e_ps, e_grouped, e_codes, e_scales = {}, {}, {}, {}
-        x_grouped, x_codes, x_scales, w_grouped = {}, {}, {}, {}
+        x_ps, w_ps, x_grouped, x_codes, x_scales, w_grouped = {}, {}, {}, {}, {}, {}
         v_ps, v_grouped, v_codes, v_scales, o_ps, o_sb = {}, {}, {}, {}, {}, {}
 
         warm = const.tile([P, 1], F32, name="warm")
@@ -119,19 +122,27 @@ def tile_attentionforonnx_pa_kernel(tc, q_u, k, matrix_bd, x, Wv, bv, out):
             if i < H:
                 nc.sync.dma_start(out=w_raw[:, i, :], in_=Wv[i * HD : (i + 1) * HD, :])
 
-        def regroup_rows(rows, grouped):
+        def transpose_rows(rows, t_ps):
             words = rows.bitcast(F32)
-            t_ps = psum_t.tile([P, 2 * E_PASSES, P], F32, name="t_ps", tag="tp")
             for g in range(2 * E_PASSES):
                 nc.tensor.transpose(t_ps[:, g, :], words[:, g * P : (g + 1) * P], ident_f32[:])
+
+        def regroup_rows(t_ps, grouped):
             nc.scalar.copy(out=grouped, in_=t_ps[:].rearrange("p (c u) n -> p c n u", u=2))
+
+        def transpose_x(b, r):
+            if b == 0:
+                x_ps[b, r] = psum_mx.tile([P, 2 * E_PASSES, P], F32, name="x_ps", tag="mx")
+            else:
+                x_ps[b, r] = psum_t.tile([P, 2 * E_PASSES, P], F32, name="x_ps", tag="tp")
+            transpose_rows(x_raw[b][:, r, :], x_ps[b, r])
 
         def regroup_x(b, r):
             if r == 0:
                 x_grouped[b] = work.tile(
                     [P, PACK, E_PASSES, P, 2], F32, name="x_grouped", bufs=2, align_bytes=64
                 )
-            regroup_rows(x_raw[b][:, r, :], x_grouped[b][:, r])
+            regroup_rows(x_ps[b, r], x_grouped[b][:, r])
 
         def quantise_x(b):
             x_codes[b] = work.tile([P, PACK, E_PASSES, P], U32, name="x_codes", bufs=2, align_bytes=64)
@@ -142,9 +153,13 @@ def tile_attentionforonnx_pa_kernel(tc, q_u, k, matrix_bd, x, Wv, bv, out):
                 in_=x_grouped[b][:].rearrange("p r c n u -> p (r c n u)").bitcast(BF16),
             )
 
+        def transpose_w(h):
+            w_ps[h] = psum_t.tile([P, 2 * E_PASSES, P], F32, name="w_ps", tag="tp")
+            transpose_rows(w_raw[:, h, :], w_ps[h])
+
         def regroup_w(h):
             w_grouped[h] = work.tile([P, E_PASSES, P, 2], F32, name="w_grouped", bufs=2, align_bytes=64)
-            regroup_rows(w_raw[:, h, :], w_grouped[h][:])
+            regroup_rows(w_ps[h], w_grouped[h][:])
 
         def quantise_w(h):
             nc.vector.quantize_mx(
@@ -189,21 +204,32 @@ def tile_attentionforonnx_pa_kernel(tc, q_u, k, matrix_bd, x, Wv, bv, out):
         def transpose_qk(i):
             g = i // GROUP
             cols = slice((i % GROUP) * HD, (i % GROUP + 1) * HD)
-            qk_ps = psum_t.tile([P, 2, T], BF16, name="qk_ps", tag="tp")
+            qk_ps[i] = psum_t.tile([P, 2, T], BF16, name="qk_ps", tag="tp")
             for a in range(TT):
-                nc.tensor.transpose(qk_ps[:, 1, a * P : (a + 1) * P], k_raw[g][:, a, cols], ident_bf[:])
+                nc.tensor.transpose(qk_ps[i][:, 1, a * P : (a + 1) * P], k_raw[g][:, a, cols], ident_bf[:])
             for a in range(TT):
-                nc.tensor.transpose(qk_ps[:, 0, a * P : (a + 1) * P], q_raw[g][:, a, cols], ident_bf[:])
+                nc.tensor.transpose(qk_ps[i][:, 0, a * P : (a + 1) * P], q_raw[g][:, a, cols], ident_bf[:])
+
+        def copy_qk(i):
             qk_t[i] = work.tile([P, 2, T], BF16, name="qk_t")
-            nc.scalar.copy(out=qk_t[i][:], in_=qk_ps[:])
+            nc.scalar.copy(
+                out=qk_t[i][:].rearrange("p s t -> p (s t)").bitcast(F32),
+                in_=qk_ps[i][:].rearrange("p s t -> p (s t)").bitcast(F32),
+            )
 
         def content_scores(n):
             i, a = n // TT, n % TT
-            ac_ps[n] = psum_ac.tile([P, T], F32, name="ac_ps")
-            nc.tensor.matmul(
-                ac_ps[n][:], lhsT=qk_t[i][:, 0, a * P : (a + 1) * P], rhs=qk_t[i][:, 1, :],
-                start=True, stop=True,
-            )
+            lhsT, rhs = qk_t[i][:, 0, a * P : (a + 1) * P], qk_t[i][:, 1, :]
+            if added_on_tensor(n):
+                sum_ps = psum_sum.tile([P, T], F32, name="sum_ps")
+                nc.tensor.matmul(sum_ps[:], lhsT=lhsT, rhs=rhs, start=True, stop=False)
+                nc.tensor.matmul(
+                    sum_ps[:], lhsT=ident_bf[:], rhs=bd_sb[i][:, a, :], start=False, stop=True
+                )
+                summed[n] = sum_ps[:]
+            else:
+                ac_ps[n] = psum_ac.tile([P, T], F32, name="ac_ps")
+                nc.tensor.matmul(ac_ps[n][:], lhsT=lhsT, rhs=rhs, start=True, stop=True)
 
         def add_shifted(n):
             i, a = n // TT, n % TT
@@ -211,17 +237,7 @@ def tile_attentionforonnx_pa_kernel(tc, q_u, k, matrix_bd, x, Wv, bv, out):
                 score[i] = work.tile([P, TT, T], F32, name="score")
                 row_max[i] = work.tile([P, TT], F32, name="row_max")
                 neg_max[i] = work.tile([P, TT], F32, name="neg_max")
-            if added_on_tensor(n):
-                sum_ps = psum_sum.tile([P, T], F32, name="sum_ps")
-                nc.tensor.matmul(
-                    sum_ps[:], lhsT=qk_t[i][:, 0, a * P : (a + 1) * P], rhs=qk_t[i][:, 1, :],
-                    start=True, stop=False,
-                )
-                nc.tensor.matmul(
-                    sum_ps[:], lhsT=ident_bf[:], rhs=bd_sb[i][:, a, :], start=False, stop=True
-                )
-                summed[n] = sum_ps[:]
-            else:
+            if n not in summed:
                 summed[n] = score[i][:, a, :]
                 nc.vector.tensor_tensor(
                     out=summed[n], in0=ac_ps[n][:], in1=bd_sb[i][:, a, :], op=ALU.add
@@ -273,8 +289,8 @@ def tile_attentionforonnx_pa_kernel(tc, q_u, k, matrix_bd, x, Wv, bv, out):
         def quantise_e(m):
             i = m // 2
             if m % 2 == 0:
-                e_codes[i] = work.tile([P, T], U32, name="e_codes", bufs=6, align_bytes=64)
-                e_scales[i] = work.tile([P, T], U8, name="e_scales", bufs=6, align_bytes=64)
+                e_codes[i] = work.tile([P, T], U32, name="e_codes", bufs=7, align_bytes=64)
+                e_scales[i] = work.tile([P, T], U8, name="e_scales", bufs=7, align_bytes=64)
             queries = slice((m % 2) * 2 * P, (m % 2 + 1) * 2 * P)
             nc.vector.quantize_mx(
                 out=e_codes[i][:, queries].bitcast(FP8X4),
@@ -320,71 +336,83 @@ def tile_attentionforonnx_pa_kernel(tc, q_u, k, matrix_bd, x, Wv, bv, out):
         request_x(0)
         request_head(1)
         request_group(1)
-        for n in range(-QK_LEAD, N_TILES + NORMALISE_LAG - 1):
+        for n in range(QK_LAG, N_TILES + ATTEND_LAG - 1):
             i = unit(n, TT, N_HEADS)
             if i is not None:
                 request_head(i + 2)
                 if i % GROUP == 0:
                     request_group(i // GROUP + 2)
-                if (i + X_AHEAD) % H == 0:
-                    request_x((i + X_AHEAD) // H)
+                if i == H // 2:
+                    request_x(1)
+
+            t = unit(n - EXP_LAG, 1, N_TILES)
+            if t is not None:
+                exponentials(t)
 
             t = unit(n + 1, 1, N_TILES)
-            if t is not None and not added_on_tensor(t):
+            if t is not None:
                 content_scores(t)
+            t = unit(n - E_T_LAG, 1, N_TILES)
+            if t is not None:
+                transpose_e(t)
+            i = unit(n - ATTEND_LAG, TT, N_HEADS)
+            if i is not None:
+                attend(i)
+            for part in range(2):
+                i = unit(n - VALUE_LAG - part, TT, N_HEADS)
+                if i is not None:
+                    project_values(i, part)
+
             t = unit(n, 1, N_TILES)
             if t is not None:
                 add_shifted(t)
             t = unit(n - 1, 1, N_TILES)
             if t is not None:
                 maximum(t)
-            t = unit(n - EXP_LAG, 1, N_TILES)
-            if t is not None:
-                exponentials(t)
-            t = unit(n - E_T_LAG, 1, N_TILES)
-            if t is not None:
-                transpose_e(t)
-            m = unit(n - E_T_LAG - 2, 2, N_HALVES)
-            if m is not None:
-                regroup_e(m)
-            m = unit(n - E_T_LAG - 3, 2, N_HALVES)
+            m = unit(n - QUANT_LAG, 2, N_HALVES)
             if m is not None:
                 quantise_e(m)
-
-            i = unit(n + QK_LEAD, TT, N_HEADS)
-            if i is not None:
-                transpose_qk(i)
-            for b in range(B):
-                since = n - b * H * TT
-                if 0 <= since < 2 * TT and since % TT >= 2:
-                    regroup_x(b, 2 * (since // TT) + since % TT - 2)
-            i = unit(n - TT, TT, H)
-            if i is not None:
-                regroup_w(i)
-
-            i = unit(n - V_LAG, TT, N_HEADS)
-            if i is not None:
-                invert_sums(i)
-            b = unit(n - V_LAG + 1, H * TT, B)
-            if b is not None:
-                quantise_x(b)
-            i = unit(n - V_LAG + 1, TT, H)
-            if i is not None:
-                quantise_w(i)
-            i = unit(n - V_LAG - 2, TT, N_HEADS)
+            i = unit(n - VALUE_LAG - 3, TT, N_HEADS)
             if i is not None:
                 add_bias(i)
-            i = unit(n - V_LAG - 3, TT, N_HEADS)
+            i = unit(n - VALUE_LAG - 4, TT, N_HEADS)
             if i is not None:
                 quantise_v(i)
-
-            i = unit(n - ATTEND_LAG, TT, N_HEADS)
+            for b in range(B):
+                if n == b * H * TT + X_LAG + 2 * PACK:
+                    quantise_x(b)
+            h = unit(n - W_LAG - 2, TT, H)
+            if h is not None:
+                quantise_w(h)
+            i = unit(n - ATTEND_LAG + 1, TT, N_HEADS)
             if i is not None:
-                attend(i)
-            for part in range(2):
-                i = unit(n - V_LAG - part, TT, N_HEADS)
-                if i is not None:
-                    project_values(i, part)
-            m = unit(n - NORMALISE_LAG, 2, N_HALVES)
+                invert_sums(i)
+
+            m = unit(n - REGROUP_LAG, 2, N_HALVES)
             if m is not None:
-                normalise(m)
+                regroup_e(m)
+            i = unit(n - QK_LAG - 1, TT, N_HEADS)
+            if i is not None:
+                copy_qk(i)
+            h = unit(n - W_LAG - 1, TT, H)
+            if h is not None:
+                regroup_w(h)
+            for b in range(B):
+                r = unit(n - b * H * TT - X_LAG - 1, 2, PACK)
+                if r is not None:
+                    regroup_x(b, r)
+            for part in range(2):
+                i = unit(n - ATTEND_LAG - 1 - part, TT, N_HEADS)
+                if i is not None:
+                    normalise(2 * i + part)
+
+            i = unit(n - QK_LAG, TT, N_HEADS)
+            if i is not None:
+                transpose_qk(i)
+            h = unit(n - W_LAG, TT, H)
+            if h is not None:
+                transpose_w(h)
+            for b in range(B):
+                r = unit(n - b * H * TT - X_LAG, 2, PACK)
+                if r is not None:
+                    transpose_x(b, r)

@@ -29,10 +29,10 @@ N_HEADS = B * H
 N_HALVES = N_HEADS * 2
 N_TILES = N_HEADS * TT
 
-EXP_LAG = 4
-E_T_LAG = 6
-REGROUP_LAG = 9
-QUANT_LAG = 10
+EXP_LAG = 3
+E_T_LAG = 5
+REGROUP_LAG = 7
+QUANT_LAG = 8
 QK_LAG = -3
 X_LAG = 2
 W_LAG = 7
@@ -349,8 +349,11 @@ def tile_attentionforonnx_pa_kernel(tc, q_u, k, matrix_bd, x, Wv, bv, out):
             if t is not None:
                 exponentials(t)
 
+            t = unit(n, 1, N_TILES)
+            if t is not None and added_on_tensor(t):
+                content_scores(t)
             t = unit(n + 1, 1, N_TILES)
-            if t is not None:
+            if t is not None and not added_on_tensor(t):
                 content_scores(t)
             t = unit(n - E_T_LAG, 1, N_TILES)
             if t is not None:

@@ -34,10 +34,8 @@ E_T_LAG = 5
 REGROUP_LAG = 7
 QUANT_LAG = 8
 QK_LAG = -3
-X_LAG = 2
+X_START = (2, 23)
 W_LAG = 7
-VALUE_LAG = 12
-ATTEND_LAG = 18
 
 TENSOR_ADDS = 12
 
@@ -51,8 +49,16 @@ def unit(slot, period, count):
     return None
 
 
+def value_slot(i):
+    return min(4 * i + 12, 3 * i + 20)
+
+
+def attend_slot(i):
+    return value_slot(i) + 6
+
+
 def added_on_tensor(n):
-    return n % TT == 0 and 1 <= n // TT <= TENSOR_ADDS
+    return n % TT == 0 and 1 <= n // TT <= 14 and not 6 <= n // TT < 8
 
 
 def tile_attentionforonnx_pa_kernel(tc, q_u, k, matrix_bd, x, Wv, bv, out):
@@ -65,7 +71,7 @@ def tile_attentionforonnx_pa_kernel(tc, q_u, k, matrix_bd, x, Wv, bv, out):
         psum_sum = ctx.enter_context(tc.psum_pool(name="psum_sum", bufs=1))
         psum_ac = ctx.enter_context(tc.psum_pool(name="psum_ac", bufs=2))
         psum_e = ctx.enter_context(tc.psum_pool(name="psum_e", bufs=2))
-        psum_mx = ctx.enter_context(tc.psum_pool(name="psum_mx", bufs=2))
+        psum_mx = ctx.enter_context(tc.psum_pool(name="psum_mx", bufs=1))
         ctx.enter_context(tc.manual_schedule())
 
         k_raw, q_raw, x_raw, bd_sb, qk_ps, qk_t, ac_ps = {}, {}, {}, {}, {}, {}, {}
@@ -132,9 +138,9 @@ def tile_attentionforonnx_pa_kernel(tc, q_u, k, matrix_bd, x, Wv, bv, out):
 
         def transpose_x(b, r):
             if b == 0:
-                x_ps[b, r] = psum_mx.tile([P, 2 * E_PASSES, P], F32, name="x_ps", tag="mx")
+                x_ps[b, r] = psum_mx.tile([P, 2 * E_PASSES, P], F32, name="x_ps", tag="vo"[r % 2])
             else:
-                x_ps[b, r] = psum_t.tile([P, 2 * E_PASSES, P], F32, name="x_ps", tag="tp")
+                x_ps[b, r] = psum_sum.tile([P, 2 * E_PASSES, P], F32, name="x_ps", tag="sum")
             transpose_rows(x_raw[b][:, r, :], x_ps[b, r])
 
         def regroup_x(b, r):
@@ -171,7 +177,7 @@ def tile_attentionforonnx_pa_kernel(tc, q_u, k, matrix_bd, x, Wv, bv, out):
         def project_values(i, part):
             b, h = i // H, i % H
             if part == 0:
-                v_ps[i] = psum_mx.tile([P, PACK, HD], F32, name="v_ps", tag="mx")
+                v_ps[i] = psum_mx.tile([P, PACK, HD], F32, name="v_ps", tag="v")
             for j in range(2 * part, 2 * part + 2):
                 for c in range(E_PASSES):
                     nc.tensor.matmul_mx(
@@ -193,8 +199,8 @@ def tile_attentionforonnx_pa_kernel(tc, q_u, k, matrix_bd, x, Wv, bv, out):
             )
 
         def quantise_v(i):
-            v_codes[i] = work.tile([P, HD], U32, name="v_codes", align_bytes=64)
-            v_scales[i] = work.tile([P, HD], U8, name="v_scales", align_bytes=64)
+            v_codes[i] = work.tile([P, HD], U32, name="v_codes", bufs=5, align_bytes=64)
+            v_scales[i] = work.tile([P, HD], U8, name="v_scales", bufs=5, align_bytes=64)
             nc.vector.quantize_mx(
                 out=v_codes[i][:].bitcast(FP8X4),
                 scales=v_scales[i][:],
@@ -221,7 +227,7 @@ def tile_attentionforonnx_pa_kernel(tc, q_u, k, matrix_bd, x, Wv, bv, out):
             i, a = n // TT, n % TT
             lhsT, rhs = qk_t[i][:, 0, a * P : (a + 1) * P], qk_t[i][:, 1, :]
             if added_on_tensor(n):
-                sum_ps = psum_sum.tile([P, T], F32, name="sum_ps")
+                sum_ps = psum_sum.tile([P, T], F32, name="sum_ps", tag="sum")
                 nc.tensor.matmul(sum_ps[:], lhsT=lhsT, rhs=rhs, start=True, stop=False)
                 nc.tensor.matmul(
                     sum_ps[:], lhsT=ident_bf[:], rhs=bd_sb[i][:, a, :], start=False, stop=True
@@ -303,7 +309,7 @@ def tile_attentionforonnx_pa_kernel(tc, q_u, k, matrix_bd, x, Wv, bv, out):
             nc.vector.reciprocal(inv_sum[i][:], row_sum[i][:])
 
         def attend(i):
-            o_ps[i] = psum_mx.tile([P, TT, HD], F32, name="o_ps", tag="mx")
+            o_ps[i] = psum_mx.tile([P, TT, HD], F32, name="o_ps", tag="o")
             for a in range(TT):
                 nc.tensor.matmul_mx(
                     out=o_ps[i][:, a, :],
@@ -336,7 +342,7 @@ def tile_attentionforonnx_pa_kernel(tc, q_u, k, matrix_bd, x, Wv, bv, out):
         request_x(0)
         request_head(1)
         request_group(1)
-        for n in range(QK_LAG, N_TILES + ATTEND_LAG - 1):
+        for n in range(QK_LAG, attend_slot(N_HEADS - 1) + 3):
             i = unit(n, TT, N_HEADS)
             if i is not None:
                 request_head(i + 2)
@@ -358,14 +364,17 @@ def tile_attentionforonnx_pa_kernel(tc, q_u, k, matrix_bd, x, Wv, bv, out):
             t = unit(n - E_T_LAG, 1, N_TILES)
             if t is not None:
                 transpose_e(t)
-            i = unit(n - ATTEND_LAG, TT, N_HEADS)
-            if i is not None:
-                attend(i)
-            for part in range(2):
-                i = unit(n - VALUE_LAG - part, TT, N_HEADS)
-                if i is not None:
-                    project_values(i, part)
+            for i in range(N_HEADS):
+                if n == attend_slot(i):
+                    attend(i)
+            for i in range(N_HEADS):
+                for part in range(2):
+                    if n == value_slot(i) + part:
+                        project_values(i, part)
 
+            for i in range(N_HEADS):
+                if n == value_slot(i) + 2:
+                    add_bias(i)
             t = unit(n, 1, N_TILES)
             if t is not None:
                 add_shifted(t)
@@ -375,21 +384,18 @@ def tile_attentionforonnx_pa_kernel(tc, q_u, k, matrix_bd, x, Wv, bv, out):
             m = unit(n - QUANT_LAG, 2, N_HALVES)
             if m is not None:
                 quantise_e(m)
-            i = unit(n - VALUE_LAG - 3, TT, N_HEADS)
-            if i is not None:
-                add_bias(i)
-            i = unit(n - VALUE_LAG - 4, TT, N_HEADS)
-            if i is not None:
-                quantise_v(i)
+            for i in range(N_HEADS):
+                if n == value_slot(i) + 4:
+                    quantise_v(i)
             for b in range(B):
-                if n == b * H * TT + X_LAG + 2 * PACK:
+                if n == X_START[b] + 2 * PACK:
                     quantise_x(b)
             h = unit(n - W_LAG - 2, TT, H)
             if h is not None:
                 quantise_w(h)
-            i = unit(n - ATTEND_LAG + 1, TT, N_HEADS)
-            if i is not None:
-                invert_sums(i)
+            for i in range(N_HEADS):
+                if n == attend_slot(i) - 1:
+                    invert_sums(i)
 
             m = unit(n - REGROUP_LAG, 2, N_HALVES)
             if m is not None:
@@ -401,13 +407,13 @@ def tile_attentionforonnx_pa_kernel(tc, q_u, k, matrix_bd, x, Wv, bv, out):
             if h is not None:
                 regroup_w(h)
             for b in range(B):
-                r = unit(n - b * H * TT - X_LAG - 1, 2, PACK)
+                r = unit(n - X_START[b] - 1, 2, PACK)
                 if r is not None:
                     regroup_x(b, r)
-            for part in range(2):
-                i = unit(n - ATTEND_LAG - 1 - part, TT, N_HEADS)
-                if i is not None:
-                    normalise(2 * i + part)
+            for i in range(N_HEADS):
+                for part in range(2):
+                    if n == attend_slot(i) + 1 + part:
+                        normalise(2 * i + part)
 
             i = unit(n - QK_LAG, TT, N_HEADS)
             if i is not None:
@@ -416,6 +422,6 @@ def tile_attentionforonnx_pa_kernel(tc, q_u, k, matrix_bd, x, Wv, bv, out):
             if h is not None:
                 transpose_w(h)
             for b in range(B):
-                r = unit(n - b * H * TT - X_LAG, 2, PACK)
+                r = unit(n - X_START[b], 2, PACK)
                 if r is not None:
                     transpose_x(b, r)

@@ -57,6 +57,14 @@ def attend_slot(i):
     return value_slot(i) + 6
 
 
+def bias_on_gpsimd(i):
+    return i % 4 == 1
+
+
+def scaled_on_gpsimd(i):
+    return i < 13
+
+
 def added_on_tensor(n):
     return n % TT == 0 and 1 <= n // TT <= 14 and not 6 <= n // TT < 8
 
@@ -194,9 +202,17 @@ def tile_attentionforonnx_pa_kernel(tc, q_u, k, matrix_bd, x, Wv, bv, out):
             h = i % H
             v_grouped[i] = work.tile([P, HD, PACK], BF16, name="v_grouped", align_bytes=64)
             bias = bias_bc[:, h * HD : (h + 1) * HD].unsqueeze(2).to_broadcast([P, HD, PACK])
-            nc.vector.tensor_tensor(
-                out=v_grouped[i][:], in0=v_ps[i][:].rearrange("p j d -> p d j"), in1=bias, op=ALU.add
-            )
+            values = v_ps[i][:].rearrange("p j d -> p d j")
+            if bias_on_gpsimd(i):
+                v_sb = work.tile([P, HD, PACK], F32, name="v_sb", bufs=2)
+                nc.scalar.copy(out=v_sb[:], in_=values)
+                for d in range(0, HD, HD // 2):
+                    cols = slice(d, d + HD // 2)
+                    nc.gpsimd.tensor_tensor(
+                        out=v_grouped[i][:, cols], in0=v_sb[:, cols], in1=bias[:, cols], op=ALU.add
+                    )
+            else:
+                nc.vector.tensor_tensor(out=v_grouped[i][:], in0=values, in1=bias, op=ALU.add)
 
         def quantise_v(i):
             v_codes[i] = work.tile([P, HD], U32, name="v_codes", bufs=5, align_bytes=64)
@@ -321,21 +337,29 @@ def tile_attentionforonnx_pa_kernel(tc, q_u, k, matrix_bd, x, Wv, bv, out):
                     stop=True,
                 )
 
-        def normalise(m):
-            i = m // 2
-            if m % 2 == 0:
-                o_sb[i] = work.tile([P, TT, HD], F32, name="o_sb")
-            for a in range(2 * (m % 2), 2 * (m % 2) + 2):
-                nc.scalar.activation(
-                    out=o_sb[i][:, a, :], in_=o_ps[i][:, a, :], func=ACT.Copy,
-                    scale=inv_sum[i][:, a : a + 1],
-                )
-            if m % 2 == 1:
-                b, h = i // H, i % H
-                nc.sync.dma_start(
-                    out=out[b].rearrange("(a p) e -> p a e", p=P)[:, :, h * HD : (h + 1) * HD],
-                    in_=o_sb[i][:],
-                )
+        def normalise(i, a):
+            nc.scalar.activation(
+                out=o_sb[i][:, a, :], in_=o_ps[i][:, a, :], func=ACT.Copy,
+                scale=inv_sum[i][:, a : a + 1],
+            )
+
+        def copy_outputs(i):
+            o_sb[i] = work.tile([P, TT, HD], F32, name="o_sb", bufs=4)
+            if scaled_on_gpsimd(i):
+                nc.scalar.copy(out=o_sb[i][:], in_=o_ps[i][:])
+
+        def scale_outputs(i, a):
+            nc.gpsimd.tensor_scalar(
+                out=o_sb[i][:, a, :], in0=o_sb[i][:, a, :], scalar1=inv_sum[i][:, a : a + 1],
+                scalar2=0.0, op0=ALU.mult, op1=ALU.add,
+            )
+
+        def store_outputs(i):
+            b, h = i // H, i % H
+            nc.sync.dma_start(
+                out=out[b].rearrange("(a p) e -> p a e", p=P)[:, :, h * HD : (h + 1) * HD],
+                in_=o_sb[i][:],
+            )
 
         request_group(0)
         request_head(0)
@@ -411,9 +435,20 @@ def tile_attentionforonnx_pa_kernel(tc, q_u, k, matrix_bd, x, Wv, bv, out):
                 if r is not None:
                     regroup_x(b, r)
             for i in range(N_HEADS):
-                for part in range(2):
-                    if n == attend_slot(i) + 1 + part:
-                        normalise(2 * i + part)
+                since = n - attend_slot(i) - 1
+                if since == 0:
+                    copy_outputs(i)
+                if scaled_on_gpsimd(i):
+                    if 1 <= since <= TT:
+                        scale_outputs(i, since - 1)
+                    if since == TT:
+                        store_outputs(i)
+                else:
+                    if 0 <= since < 2:
+                        normalise(i, 2 * since)
+                        normalise(i, 2 * since + 1)
+                    if since == 1:
+                        store_outputs(i)
 
             i = unit(n - QK_LAG, TT, N_HEADS)
             if i is not None:

@@ -33,8 +33,9 @@ EXP_LAG = 3
 E_T_LAG = 5
 REGROUP_LAG = 7
 QUANT_LAG = 8
+LAST_TILE_LAG = 6
 QK_LAG = -3
-X_START = (2, 23)
+X_START = (0, 23)
 W_LAG = 7
 
 TENSOR_ADDS = 12
@@ -50,19 +51,19 @@ def unit(slot, period, count):
 
 
 def value_slot(i):
-    return min(4 * i + 12, 3 * i + 20)
+    return min(4 * i + 12, 3 * i + 18)
 
 
 def attend_slot(i):
-    return value_slot(i) + 6
+    return max(value_slot(i) + 6, 4 * i + 11)
 
 
 def bias_on_gpsimd(i):
-    return i % 4 == 1
+    return i % 3 == 1 and i < 14
 
 
 def scaled_on_gpsimd(i):
-    return i < 13
+    return i < 14
 
 
 def added_on_tensor(n):
@@ -126,13 +127,18 @@ def tile_attentionforonnx_pa_kernel(tc, q_u, k, matrix_bd, x, Wv, bv, out):
                 in_=x[b].rearrange("(u p e) f -> p u (e f)", u=2, p=P),
             )
 
-        def request_head(i):
+        def request_head(i, first=0, last=TT):
             if i >= N_HEADS:
                 return
             window = bd_flat[i // H, i % H, T - 1 : T - 1 + T * (REL - 1)]
             window = window.rearrange("(a p c) -> p a c", a=TT, p=P)
-            bd_sb[i] = work.tile([P, TT, T], BF16, name="bd_sb", bufs=4)
-            nc.sync.dma_start(out=bd_sb[i][:], in_=window[:, :, 0:T])
+            if first == 0:
+                bd_sb[i] = work.tile([P, TT, T], BF16, name="bd_sb", bufs=4)
+            nc.sync.dma_start(
+                out=bd_sb[i][:, first:last], in_=window[:, first:last, 0:T]
+            )
+            if last < TT:
+                return
             if i < H:
                 nc.sync.dma_start(out=w_raw[:, i, :], in_=Wv[i * HD : (i + 1) * HD, :])
 
@@ -271,19 +277,22 @@ def tile_attentionforonnx_pa_kernel(tc, q_u, k, matrix_bd, x, Wv, bv, out):
                 out=row_max[i][:, a : a + 1], in_=summed[n], axis=mybir.AxisListType.X,
                 op=ALU.max,
             )
-            nc.gpsimd.tensor_scalar(
-                out=neg_max[i][:, a : a + 1], in0=row_max[i][:, a : a + 1], scalar1=-SCALE,
-                scalar2=0.0, op0=ALU.mult, op1=ALU.add,
-            )
+
+        def scale_maximum(n):
+            i, a = n // TT, n % TT
+            nc.scalar.mul(neg_max[i][:, a : a + 1], row_max[i][:, a : a + 1], -SCALE)
 
         def exponentials(n):
             i, a = n // TT, n % TT
             if a == 0:
                 e_sb[i] = work.tile([P, TT, T], BF16, name="e_sb")
-                row_sum[i] = work.tile([P, TT], F32, name="row_sum", bufs=4)
+                if i % GROUP == 0:
+                    row_sum[i // GROUP] = work.tile([P, GROUP * TT], F32, name="row_sum", bufs=4)
+            column = n % (GROUP * TT)
             nc.scalar.activation(
                 out=e_sb[i][:, a, :], in_=summed[n], func=ACT.Exp,
-                bias=neg_max[i][:, a : a + 1], scale=SCALE, accum_out=row_sum[i][:, a : a + 1],
+                bias=neg_max[i][:, a : a + 1], scale=SCALE,
+                accum_out=row_sum[i // GROUP][:, column : column + 1],
             )
 
         def transpose_e(n):
@@ -298,31 +307,32 @@ def tile_attentionforonnx_pa_kernel(tc, q_u, k, matrix_bd, x, Wv, bv, out):
                     ident_f32[:],
                 )
 
-        def regroup_e(m):
-            i = m // 2
-            if m % 2 == 0:
+        def regroup_e(i, first, last):
+            if first == 0:
                 e_grouped[i] = work.tile([P, T * PACK], BF16, name="e_grouped", align_bytes=64)
             words = e_grouped[i][:].bitcast(F32).rearrange("p (t u) -> p t u", u=2)
+            in_half = slice((first % 2) * P, (first % 2 + last - first) * P)
             nc.scalar.copy(
-                out=words[:, (m % 2) * 2 * P : (m % 2 + 1) * 2 * P, :],
-                in_=e_ps[m][:].rearrange("p u t -> p t u"),
+                out=words[:, first * P : last * P, :],
+                in_=e_ps[2 * i + first // 2][:, :, in_half].rearrange("p u t -> p t u"),
             )
 
-        def quantise_e(m):
-            i = m // 2
-            if m % 2 == 0:
-                e_codes[i] = work.tile([P, T], U32, name="e_codes", bufs=7, align_bytes=64)
-                e_scales[i] = work.tile([P, T], U8, name="e_scales", bufs=7, align_bytes=64)
-            queries = slice((m % 2) * 2 * P, (m % 2 + 1) * 2 * P)
+        def quantise_e(i, first, last):
+            if first == 0:
+                e_codes[i] = work.tile([P, T], U32, name="e_codes", bufs=6, align_bytes=64)
+                e_scales[i] = work.tile([P, T], U8, name="e_scales", bufs=6, align_bytes=64)
+            queries = slice(first * P, last * P)
             nc.vector.quantize_mx(
                 out=e_codes[i][:, queries].bitcast(FP8X4),
                 scales=e_scales[i][:, queries],
-                in_=e_grouped[i][:, (m % 2) * 2 * P * PACK : (m % 2 + 1) * 2 * P * PACK],
+                in_=e_grouped[i][:, first * P * PACK : last * P * PACK],
             )
 
-        def invert_sums(i):
-            inv_sum[i] = work.tile([P, TT], F32, name="inv_sum", bufs=4)
-            nc.vector.reciprocal(inv_sum[i][:], row_sum[i][:])
+        def invert_sums(g):
+            sums_inv = work.tile([P, GROUP * TT], F32, name="inv_sum", bufs=4)
+            nc.vector.reciprocal(sums_inv[:], row_sum[g][:])
+            for j in range(GROUP):
+                inv_sum[g * GROUP + j] = sums_inv[:, j * TT : (j + 1) * TT]
 
         def attend(i):
             o_ps[i] = psum_mx.tile([P, TT, HD], F32, name="o_ps", tag="o")
@@ -338,10 +348,15 @@ def tile_attentionforonnx_pa_kernel(tc, q_u, k, matrix_bd, x, Wv, bv, out):
                 )
 
         def normalise(i, a):
-            nc.scalar.activation(
-                out=o_sb[i][:, a, :], in_=o_ps[i][:, a, :], func=ACT.Copy,
-                scale=inv_sum[i][:, a : a + 1],
-            )
+            if i == N_HEADS - 1:
+                nc.vector.tensor_scalar_mul(
+                    out=o_sb[i][:, a, :], in0=o_ps[i][:, a, :], scalar1=inv_sum[i][:, a : a + 1]
+                )
+            else:
+                nc.scalar.activation(
+                    out=o_sb[i][:, a, :], in_=o_ps[i][:, a, :], func=ACT.Copy,
+                    scale=inv_sum[i][:, a : a + 1],
+                )
 
         def copy_outputs(i):
             o_sb[i] = work.tile([P, TT, HD], F32, name="o_sb", bufs=4)
@@ -362,8 +377,9 @@ def tile_attentionforonnx_pa_kernel(tc, q_u, k, matrix_bd, x, Wv, bv, out):
             )
 
         request_group(0)
-        request_head(0)
+        request_head(0, 0, 2)
         request_x(0)
+        request_head(0, 2, TT)
         request_head(1)
         request_group(1)
         for n in range(QK_LAG, attend_slot(N_HEADS - 1) + 3):
@@ -378,6 +394,9 @@ def tile_attentionforonnx_pa_kernel(tc, q_u, k, matrix_bd, x, Wv, bv, out):
             t = unit(n - EXP_LAG, 1, N_TILES)
             if t is not None:
                 exponentials(t)
+            t = unit(n - EXP_LAG + 1, 1, N_TILES)
+            if t is not None:
+                scale_maximum(t)
 
             t = unit(n, 1, N_TILES)
             if t is not None and added_on_tensor(t):
@@ -405,9 +424,12 @@ def tile_attentionforonnx_pa_kernel(tc, q_u, k, matrix_bd, x, Wv, bv, out):
             t = unit(n - 1, 1, N_TILES)
             if t is not None:
                 maximum(t)
-            m = unit(n - QUANT_LAG, 2, N_HALVES)
+            m = unit(n - QUANT_LAG, 2, N_HALVES - 1)
             if m is not None:
-                quantise_e(m)
+                quantise_e(m // 2, 2 * (m % 2), 2 * (m % 2) + 2)
+            t = n - LAST_TILE_LAG - 1
+            if N_TILES - 2 <= t < N_TILES:
+                quantise_e(N_HEADS - 1, t % TT, t % TT + 1)
             for i in range(N_HEADS):
                 if n == value_slot(i) + 4:
                     quantise_v(i)
@@ -418,12 +440,15 @@ def tile_attentionforonnx_pa_kernel(tc, q_u, k, matrix_bd, x, Wv, bv, out):
             if h is not None:
                 quantise_w(h)
             for i in range(N_HEADS):
-                if n == attend_slot(i) - 1:
-                    invert_sums(i)
+                if i % GROUP == 0 and n == attend_slot(i) - 1:
+                    invert_sums(i // GROUP)
 
-            m = unit(n - REGROUP_LAG, 2, N_HALVES)
+            m = unit(n - REGROUP_LAG, 2, N_HALVES - 1)
             if m is not None:
-                regroup_e(m)
+                regroup_e(m // 2, 2 * (m % 2), 2 * (m % 2) + 2)
+            t = n - LAST_TILE_LAG
+            if N_TILES - 2 <= t < N_TILES:
+                regroup_e(N_HEADS - 1, t % TT, t % TT + 1)
             i = unit(n - QK_LAG - 1, TT, N_HEADS)
             if i is not None:
                 copy_qk(i)

@@ -59,11 +59,15 @@ def attend_slot(i):
 
 
 def bias_on_gpsimd(i):
-    return i % 3 == 1 and i < 14
+    return i % 3 == 1 and i < 12
 
 
 def scaled_on_gpsimd(i):
     return i < 14
+
+
+def qk_pieces(i):
+    return ((0, TT + 1), (TT + 1, 2 * TT)) if i == 0 else ((0, 2 * TT),)
 
 
 def added_on_tensor(n):
@@ -229,25 +233,30 @@ def tile_attentionforonnx_pa_kernel(tc, q_u, k, matrix_bd, x, Wv, bv, out):
                 in_=v_grouped[i][:].rearrange("p d j -> p (d j)"),
             )
 
-        def transpose_qk(i):
+        def transpose_qk(i, first, last):
             g = i // GROUP
             cols = slice((i % GROUP) * HD, (i % GROUP + 1) * HD)
-            qk_ps[i] = psum_t.tile([P, 2, T], BF16, name="qk_ps", tag="tp")
-            for a in range(TT):
-                nc.tensor.transpose(qk_ps[i][:, 1, a * P : (a + 1) * P], k_raw[g][:, a, cols], ident_bf[:])
-            for a in range(TT):
-                nc.tensor.transpose(qk_ps[i][:, 0, a * P : (a + 1) * P], q_raw[g][:, a, cols], ident_bf[:])
+            pool, tag = (psum_t, "tp") if first == 0 else (psum_sum, "sum")
+            qk_ps[i, first] = pool.tile([P, (last - first) * P], BF16, name="qk_ps", tag=tag)
+            for piece in range(first, last):
+                rows = k_raw[g] if piece < TT else q_raw[g]
+                nc.tensor.transpose(
+                    qk_ps[i, first][:, (piece - first) * P : (piece - first + 1) * P],
+                    rows[:, piece % TT, cols],
+                    ident_bf[:],
+                )
 
-        def copy_qk(i):
-            qk_t[i] = work.tile([P, 2, T], BF16, name="qk_t")
+        def copy_qk(i, first, last):
+            if first == 0:
+                qk_t[i] = work.tile([P, 2 * T], BF16, name="qk_t")
             nc.scalar.copy(
-                out=qk_t[i][:].rearrange("p s t -> p (s t)").bitcast(F32),
-                in_=qk_ps[i][:].rearrange("p s t -> p (s t)").bitcast(F32),
+                out=qk_t[i][:, first * P : last * P].bitcast(F32),
+                in_=qk_ps[i, first][:].bitcast(F32),
             )
 
         def content_scores(n):
             i, a = n // TT, n % TT
-            lhsT, rhs = qk_t[i][:, 0, a * P : (a + 1) * P], qk_t[i][:, 1, :]
+            lhsT, rhs = qk_t[i][:, T + a * P : T + (a + 1) * P], qk_t[i][:, :T]
             if added_on_tensor(n):
                 sum_ps = psum_sum.tile([P, T], F32, name="sum_ps", tag="sum")
                 nc.tensor.matmul(sum_ps[:], lhsT=lhsT, rhs=rhs, start=True, stop=False)
@@ -335,7 +344,8 @@ def tile_attentionforonnx_pa_kernel(tc, q_u, k, matrix_bd, x, Wv, bv, out):
                 inv_sum[g * GROUP + j] = sums_inv[:, j * TT : (j + 1) * TT]
 
         def attend(i):
-            o_ps[i] = psum_mx.tile([P, TT, HD], F32, name="o_ps", tag="o")
+            tag = "o" if i < N_HEADS - 1 else "v"
+            o_ps[i] = psum_mx.tile([P, TT, HD], F32, name="o_ps", tag=tag)
             for a in range(TT):
                 nc.tensor.matmul_mx(
                     out=o_ps[i][:, a, :],
@@ -369,11 +379,11 @@ def tile_attentionforonnx_pa_kernel(tc, q_u, k, matrix_bd, x, Wv, bv, out):
                 scalar2=0.0, op0=ALU.mult, op1=ALU.add,
             )
 
-        def store_outputs(i):
+        def store_outputs(i, first, last):
             b, h = i // H, i % H
             nc.sync.dma_start(
-                out=out[b].rearrange("(a p) e -> p a e", p=P)[:, :, h * HD : (h + 1) * HD],
-                in_=o_sb[i][:],
+                out=out[b].rearrange("(a p) e -> p a e", p=P)[:, first:last, h * HD : (h + 1) * HD],
+                in_=o_sb[i][:, first:last],
             )
 
         request_group(0)
@@ -398,9 +408,6 @@ def tile_attentionforonnx_pa_kernel(tc, q_u, k, matrix_bd, x, Wv, bv, out):
             if t is not None:
                 scale_maximum(t)
 
-            t = unit(n, 1, N_TILES)
-            if t is not None and added_on_tensor(t):
-                content_scores(t)
             t = unit(n + 1, 1, N_TILES)
             if t is not None and not added_on_tensor(t):
                 content_scores(t)
@@ -414,6 +421,10 @@ def tile_attentionforonnx_pa_kernel(tc, q_u, k, matrix_bd, x, Wv, bv, out):
                 for part in range(2):
                     if n == value_slot(i) + part:
                         project_values(i, part)
+
+            t = unit(n, 1, N_TILES)
+            if t is not None and added_on_tensor(t):
+                content_scores(t)
 
             for i in range(N_HEADS):
                 if n == value_slot(i) + 2:
@@ -451,7 +462,8 @@ def tile_attentionforonnx_pa_kernel(tc, q_u, k, matrix_bd, x, Wv, bv, out):
                 regroup_e(N_HEADS - 1, t % TT, t % TT + 1)
             i = unit(n - QK_LAG - 1, TT, N_HEADS)
             if i is not None:
-                copy_qk(i)
+                for first, last in qk_pieces(i):
+                    copy_qk(i, first, last)
             h = unit(n - W_LAG - 1, TT, H)
             if h is not None:
                 regroup_w(h)
@@ -467,17 +479,17 @@ def tile_attentionforonnx_pa_kernel(tc, q_u, k, matrix_bd, x, Wv, bv, out):
                     if 1 <= since <= TT:
                         scale_outputs(i, since - 1)
                     if since == TT:
-                        store_outputs(i)
+                        store_outputs(i, 0, TT)
                 else:
                     if 0 <= since < 2:
                         normalise(i, 2 * since)
                         normalise(i, 2 * since + 1)
-                    if since == 1:
-                        store_outputs(i)
+                        store_outputs(i, 2 * since, 2 * since + 2)
 
             i = unit(n - QK_LAG, TT, N_HEADS)
             if i is not None:
-                transpose_qk(i)
+                for first, last in qk_pieces(i):
+                    transpose_qk(i, first, last)
             h = unit(n - W_LAG, TT, H)
             if h is not None:
                 transpose_w(h)

@@ -51,19 +51,11 @@ def unit(slot, period, count):
 
 
 def value_slot(i):
-    return min(4 * i + 12, 3 * i + 18)
+    return min(4 * i + 12, 3 * i + 20)
 
 
 def attend_slot(i):
     return max(value_slot(i) + 6, 4 * i + 11)
-
-
-def bias_on_gpsimd(i):
-    return i % 3 == 1 and i < 12
-
-
-def scaled_on_gpsimd(i):
-    return i < 14
 
 
 def qk_pieces(i):
@@ -212,17 +204,9 @@ def tile_attentionforonnx_pa_kernel(tc, q_u, k, matrix_bd, x, Wv, bv, out):
             h = i % H
             v_grouped[i] = work.tile([P, HD, PACK], BF16, name="v_grouped", align_bytes=64)
             bias = bias_bc[:, h * HD : (h + 1) * HD].unsqueeze(2).to_broadcast([P, HD, PACK])
-            values = v_ps[i][:].rearrange("p j d -> p d j")
-            if bias_on_gpsimd(i):
-                v_sb = work.tile([P, HD, PACK], F32, name="v_sb", bufs=2)
-                nc.scalar.copy(out=v_sb[:], in_=values)
-                for d in range(0, HD, HD // 2):
-                    cols = slice(d, d + HD // 2)
-                    nc.gpsimd.tensor_tensor(
-                        out=v_grouped[i][:, cols], in0=v_sb[:, cols], in1=bias[:, cols], op=ALU.add
-                    )
-            else:
-                nc.vector.tensor_tensor(out=v_grouped[i][:], in0=values, in1=bias, op=ALU.add)
+            nc.vector.tensor_tensor(
+                out=v_grouped[i][:], in0=v_ps[i][:].rearrange("p j d -> p d j"), in1=bias, op=ALU.add
+            )
 
         def quantise_v(i):
             v_codes[i] = work.tile([P, HD], U32, name="v_codes", bufs=5, align_bytes=64)
@@ -358,6 +342,8 @@ def tile_attentionforonnx_pa_kernel(tc, q_u, k, matrix_bd, x, Wv, bv, out):
                 )
 
         def normalise(i, a):
+            if a == 0:
+                o_sb[i] = work.tile([P, TT, HD], F32, name="o_sb", bufs=4)
             if i == N_HEADS - 1:
                 nc.vector.tensor_scalar_mul(
                     out=o_sb[i][:, a, :], in0=o_ps[i][:, a, :], scalar1=inv_sum[i][:, a : a + 1]
@@ -367,17 +353,6 @@ def tile_attentionforonnx_pa_kernel(tc, q_u, k, matrix_bd, x, Wv, bv, out):
                     out=o_sb[i][:, a, :], in_=o_ps[i][:, a, :], func=ACT.Copy,
                     scale=inv_sum[i][:, a : a + 1],
                 )
-
-        def copy_outputs(i):
-            o_sb[i] = work.tile([P, TT, HD], F32, name="o_sb", bufs=4)
-            if scaled_on_gpsimd(i):
-                nc.scalar.copy(out=o_sb[i][:], in_=o_ps[i][:])
-
-        def scale_outputs(i, a):
-            nc.gpsimd.tensor_scalar(
-                out=o_sb[i][:, a, :], in0=o_sb[i][:, a, :], scalar1=inv_sum[i][:, a : a + 1],
-                scalar2=0.0, op0=ALU.mult, op1=ALU.add,
-            )
 
         def store_outputs(i, first, last):
             b, h = i // H, i % H
@@ -472,19 +447,14 @@ def tile_attentionforonnx_pa_kernel(tc, q_u, k, matrix_bd, x, Wv, bv, out):
                 if r is not None:
                     regroup_x(b, r)
             for i in range(N_HEADS):
-                since = n - attend_slot(i) - 1
-                if since == 0:
-                    copy_outputs(i)
-                if scaled_on_gpsimd(i):
-                    if 1 <= since <= TT:
-                        scale_outputs(i, since - 1)
-                    if since == TT:
-                        store_outputs(i, 0, TT)
-                else:
-                    if 0 <= since < 2:
-                        normalise(i, 2 * since)
-                        normalise(i, 2 * since + 1)
-                        store_outputs(i, 2 * since, 2 * since + 2)
+                for half in range(2):
+                    if n == attend_slot(i) + 1 + half:
+                        normalise(i, 2 * half)
+                        normalise(i, 2 * half + 1)
+                        if i >= N_HEADS - 2:
+                            store_outputs(i, 2 * half, 2 * half + 2)
+                        elif half == 1:
+                            store_outputs(i, 0, TT)
 
             i = unit(n - QK_LAG, TT, N_HEADS)
             if i is not None:

@@ -160,13 +160,15 @@ def tile_attentionforonnx_pa_kernel(tc, q_u, k, matrix_bd, x, Wv, bv, out):
                 )
             regroup_rows(x_ps[b, r], x_grouped[b][:, r])
 
-        def quantise_x(b):
-            x_codes[b] = work.tile([P, PACK, E_PASSES, P], U32, name="x_codes", bufs=2, align_bytes=64)
-            x_scales[b] = work.tile([P, PACK, E_PASSES, P], U8, name="x_scales", bufs=2, align_bytes=64)
+        def quantise_x(b, first, last):
+            if first == 0:
+                x_codes[b] = work.tile([P, PACK, E_PASSES, P], U32, name="x_codes", bufs=2, align_bytes=64)
+                x_scales[b] = work.tile([P, PACK, E_PASSES, P], U8, name="x_scales", bufs=2, align_bytes=64)
+            rows = slice(first, last)
             nc.vector.quantize_mx(
-                out=x_codes[b][:].rearrange("p r c n -> p (r c n)").bitcast(FP8X4),
-                scales=x_scales[b][:].rearrange("p r c n -> p (r c n)"),
-                in_=x_grouped[b][:].rearrange("p r c n u -> p (r c n u)").bitcast(BF16),
+                out=x_codes[b][:, rows].rearrange("p r c n -> p (r c n)").bitcast(FP8X4),
+                scales=x_scales[b][:, rows].rearrange("p r c n -> p (r c n)"),
+                in_=x_grouped[b][:, rows].rearrange("p r c n u -> p (r c n u)").bitcast(BF16),
             )
 
         def transpose_w(h):
@@ -270,10 +272,10 @@ def tile_attentionforonnx_pa_kernel(tc, q_u, k, matrix_bd, x, Wv, bv, out):
                 out=row_max[i][:, a : a + 1], in_=summed[n], axis=mybir.AxisListType.X,
                 op=ALU.max,
             )
-
-        def scale_maximum(n):
-            i, a = n // TT, n % TT
-            nc.scalar.mul(neg_max[i][:, a : a + 1], row_max[i][:, a : a + 1], -SCALE)
+            nc.gpsimd.tensor_scalar(
+                out=neg_max[i][:, a : a + 1], in0=row_max[i][:, a : a + 1], scalar1=-SCALE,
+                scalar2=0.0, op0=ALU.mult, op1=ALU.add,
+            )
 
         def exponentials(n):
             i, a = n // TT, n % TT
@@ -379,9 +381,6 @@ def tile_attentionforonnx_pa_kernel(tc, q_u, k, matrix_bd, x, Wv, bv, out):
             t = unit(n - EXP_LAG, 1, N_TILES)
             if t is not None:
                 exponentials(t)
-            t = unit(n - EXP_LAG + 1, 1, N_TILES)
-            if t is not None:
-                scale_maximum(t)
 
             t = unit(n + 1, 1, N_TILES)
             if t is not None and not added_on_tensor(t):
@@ -420,8 +419,10 @@ def tile_attentionforonnx_pa_kernel(tc, q_u, k, matrix_bd, x, Wv, bv, out):
                 if n == value_slot(i) + 4:
                     quantise_v(i)
             for b in range(B):
+                if n == X_START[b] + PACK:
+                    quantise_x(b, 0, 2)
                 if n == X_START[b] + 2 * PACK:
-                    quantise_x(b)
+                    quantise_x(b, 2, PACK)
             h = unit(n - W_LAG - 2, TT, H)
             if h is not None:
                 quantise_w(h)

import math
from contextlib import ExitStack

import concourse.mybir as mybir
from concourse.masks import make_identity

F32 = mybir.dt.float32
BF16 = mybir.dt.bfloat16
U32 = mybir.dt.uint32
U8 = mybir.dt.uint8
FP8X4 = mybir.dt.float8_e4m3fn_x4
ALU = mybir.AluOpType
ACT = mybir.ActivationFunctionType

P = 128
B = 2
T = 512
E = 1024
H = 8
HD = 128
REL = 2 * T - 1
TT = T // P
PACK = 4
K_PASS = P * PACK
E_PASSES = E // K_PASS
SCALE = 1.0 / math.sqrt(HD)
GROUP = 2
N_HEADS = B * H
N_HALVES = N_HEADS * 2
N_TILES = N_HEADS * TT

EXP_LAG = 3
E_T_LAG = 5
REGROUP_LAG = 7
QUANT_LAG = 8
LAST_TILE_LAG = 6
QK_LAG = -3
X_START = (0, 23)
W_LAG = 7

TENSOR_ADDS = 12

FLOPS = 2 * B * T * E * E + 2 * 2 * B * H * T * T * HD
BYTES = 2 * (3 * B * T * E + E * E + E + B * H * T * T) + 4 * B * T * E


def unit(slot, period, count):
    if slot % period == 0 and 0 <= slot // period < count:
        return slot // period
    return None


def value_slot(i):
    return min(4 * i + 12, 3 * i + 20)


def attend_slot(i):
    return max(value_slot(i) + 6, 4 * i + 11)


def qk_pieces(i):
    return ((0, TT + 1), (TT + 1, 2 * TT)) if i == 0 else ((0, 2 * TT),)


def added_on_tensor(n):
    return n % TT == 0 and 1 <= n // TT <= 14 and not 6 <= n // TT < 8


def tile_attentionforonnx_pa_kernel(tc, q_u, k, matrix_bd, x, Wv, bv, out):
    nc = tc.nc
    with ExitStack() as ctx:
        const = ctx.enter_context(tc.tile_pool(name="const", bufs=1))
        raw = ctx.enter_context(tc.tile_pool(name="raw", bufs=2))
        work = ctx.enter_context(tc.tile_pool(name="work", bufs=3))
        psum_t = ctx.enter_context(tc.psum_pool(name="psum_t", bufs=1))
        psum_sum = ctx.enter_context(tc.psum_pool(name="psum_sum", bufs=1))
        psum_ac = ctx.enter_context(tc.psum_pool(name="psum_ac", bufs=2))
        psum_e = ctx.enter_context(tc.psum_pool(name="psum_e", bufs=2))
        psum_mx = ctx.enter_context(tc.psum_pool(name="psum_mx", bufs=1))
        ctx.enter_context(tc.manual_schedule())

        k_raw, q_raw, x_raw, bd_sb, qk_ps, qk_t, ac_ps = {}, {}, {}, {}, {}, {}, {}
        score, summed, row_max, neg_max, e_sb, row_sum, inv_sum = {}, {}, {}, {}, {}, {}, {}
        e_ps, e_grouped, e_codes, e_scales = {}, {}, {}, {}
        x_ps, w_ps, x_grouped, x_codes, x_scales, w_grouped = {}, {}, {}, {}, {}, {}
        v_ps, v_grouped, v_codes, v_scales, o_ps, o_sb = {}, {}, {}, {}, {}, {}

        warm = const.tile([P, 1], F32, name="warm")
        nc.vector.memset(warm[:], 0.0)
        nc.scalar.activation(out=warm[:], in_=warm[:], func=ACT.Exp)
        ident_bf = const.tile([P, P], BF16, name="ident_bf")
        make_identity(nc, ident_bf[:])
        ident_f32 = const.tile([P, P], F32, name="ident_f32")
        make_identity(nc, ident_f32[:])
        bias_bc = const.tile([P, E], BF16, name="bias_bc")
        nc.gpsimd.dma_start(out=bias_bc[:], in_=bv.partition_broadcast(P))
        w_raw = const.tile([P, H, E], BF16, name="w_raw")
        w_codes = const.tile([P, H, E_PASSES, P], U32, name="w_codes", align_bytes=64)
        w_scales = const.tile([P, H, E_PASSES, P], U8, name="w_scales", align_bytes=64)

        bd_flat = matrix_bd.rearrange("b h t r -> b h (t r)")

        def request_group(g):
            if g >= N_HEADS // GROUP:
                return
            b = g * GROUP // H
            cols = slice((g * GROUP % H) * HD, (g * GROUP % H + GROUP) * HD)
            k_raw[g] = raw.tile([P, TT, GROUP * HD], BF16, name="k_raw", bufs=N_HEADS // GROUP)
            q_raw[g] = raw.tile([P, TT, GROUP * HD], BF16, name="q_raw", bufs=N_HEADS // GROUP)
            nc.sync.dma_start(
                out=k_raw[g][:], in_=k[b].rearrange("(a p) h d -> p a (h d)", p=P)[:, :, cols]
            )
            nc.sync.dma_start(
                out=q_raw[g][:], in_=q_u[b].rearrange("(a p) h d -> p a (h d)", p=P)[:, :, cols]
            )

        def request_x(b):
            if b >= B:
                return
            x_raw[b] = raw.tile([P, PACK, E], BF16, name="x_raw")
            nc.sync.dma_start(
                out=x_raw[b][:].rearrange("p (u e) f -> p u (e f)", u=2),
                in_=x[b].rearrange("(u p e) f -> p u (e f)", u=2, p=P),
            )

        def request_head(i, first=0, last=TT):
            if i >= N_HEADS:
                return
            window = bd_flat[i // H, i % H, T - 1 : T - 1 + T * (REL - 1)]
            window = window.rearrange("(a p c) -> p a c", a=TT, p=P)
            if first == 0:
                bd_sb[i] = work.tile([P, TT, T], BF16, name="bd_sb", bufs=4)
            nc.sync.dma_start(
                out=bd_sb[i][:, first:last], in_=window[:, first:last, 0:T]
            )
            if last < TT:
                return
            if i < H:
                nc.sync.dma_start(out=w_raw[:, i, :], in_=Wv[i * HD : (i + 1) * HD, :])

        def transpose_rows(rows, t_ps):
            words = rows.bitcast(F32)
            for g in range(2 * E_PASSES):
                nc.tensor.transpose(t_ps[:, g, :], words[:, g * P : (g + 1) * P], ident_f32[:])

        def regroup_rows(t_ps, grouped):
            nc.scalar.copy(out=grouped, in_=t_ps[:].rearrange("p (c u) n -> p c n u", u=2))

        def transpose_x(b, r):
            if b == 0:
                x_ps[b, r] = psum_mx.tile([P, 2 * E_PASSES, P], F32, name="x_ps", tag="vo"[r % 2])
            else:
                x_ps[b, r] = psum_sum.tile([P, 2 * E_PASSES, P], F32, name="x_ps", tag="sum")
            transpose_rows(x_raw[b][:, r, :], x_ps[b, r])

        def regroup_x(b, r):
            if r == 0:
                x_grouped[b] = work.tile(
                    [P, PACK, E_PASSES, P, 2], F32, name="x_grouped", bufs=2, align_bytes=64
                )
            regroup_rows(x_ps[b, r], x_grouped[b][:, r])

        def quantise_x(b, first, last):
            if first == 0:
                x_codes[b] = work.tile([P, PACK, E_PASSES, P], U32, name="x_codes", bufs=2, align_bytes=64)
                x_scales[b] = work.tile([P, PACK, E_PASSES, P], U8, name="x_scales", bufs=2, align_bytes=64)
            rows = slice(first, last)
            nc.vector.quantize_mx(
                out=x_codes[b][:, rows].rearrange("p r c n -> p (r c n)").bitcast(FP8X4),
                scales=x_scales[b][:, rows].rearrange("p r c n -> p (r c n)"),
                in_=x_grouped[b][:, rows].rearrange("p r c n u -> p (r c n u)").bitcast(BF16),
            )

        def transpose_w(h):
            w_ps[h] = psum_t.tile([P, 2 * E_PASSES, P], F32, name="w_ps", tag="tp")
            transpose_rows(w_raw[:, h, :], w_ps[h])

        def regroup_w(h):
            w_grouped[h] = work.tile([P, E_PASSES, P, 2], F32, name="w_grouped", bufs=2, align_bytes=64)
            regroup_rows(w_ps[h], w_grouped[h][:])

        def quantise_w(h):
            nc.vector.quantize_mx(
                out=w_codes[:, h].rearrange("p c n -> p (c n)").bitcast(FP8X4),
                scales=w_scales[:, h].rearrange("p c n -> p (c n)"),
                in_=w_grouped[h][:].rearrange("p c n u -> p (c n u)").bitcast(BF16),
            )

        def project_values(i, part):
            b, h = i // H, i % H
            if part == 0:
                v_ps[i] = psum_mx.tile([P, PACK, HD], F32, name="v_ps", tag="v")
            for j in range(2 * part, 2 * part + 2):
                for c in range(E_PASSES):
                    nc.tensor.matmul_mx(
                        out=v_ps[i][:, j, :],
                        lhsT=x_codes[b][:, j, c, :].bitcast(FP8X4),
                        lhsT_scale=x_scales[b][:, j, c, :],
                        rhs=w_codes[:, h, c, :].bitcast(FP8X4),
                        rhs_scale=w_scales[:, h, c, :],
                        start=(c == 0),
                        stop=(c == E_PASSES - 1),
                    )

        def add_bias(i):
            h = i % H
            v_grouped[i] = work.tile([P, HD, PACK], BF16, name="v_grouped", align_bytes=64)
            bias = bias_bc[:, h * HD : (h + 1) * HD].unsqueeze(2).to_broadcast([P, HD, PACK])
            nc.vector.tensor_tensor(
                out=v_grouped[i][:], in0=v_ps[i][:].rearrange("p j d -> p d j"), in1=bias, op=ALU.add
            )

        def quantise_v(i):
            v_codes[i] = work.tile([P, HD], U32, name="v_codes", bufs=5, align_bytes=64)
            v_scales[i] = work.tile([P, HD], U8, name="v_scales", bufs=5, align_bytes=64)
            nc.vector.quantize_mx(
                out=v_codes[i][:].bitcast(FP8X4),
                scales=v_scales[i][:],
                in_=v_grouped[i][:].rearrange("p d j -> p (d j)"),
            )

        def transpose_qk(i, first, last):
            g = i // GROUP
            cols = slice((i % GROUP) * HD, (i % GROUP + 1) * HD)
            pool, tag = (psum_t, "tp") if first == 0 else (psum_sum, "sum")
            qk_ps[i, first] = pool.tile([P, (last - first) * P], BF16, name="qk_ps", tag=tag)
            for piece in range(first, last):
                rows = k_raw[g] if piece < TT else q_raw[g]
                nc.tensor.transpose(
                    qk_ps[i, first][:, (piece - first) * P : (piece - first + 1) * P],
                    rows[:, piece % TT, cols],
                    ident_bf[:],
                )

        def copy_qk(i, first, last):
            if first == 0:
                qk_t[i] = work.tile([P, 2 * T], BF16, name="qk_t")
            nc.scalar.copy(
                out=qk_t[i][:, first * P : last * P].bitcast(F32),
                in_=qk_ps[i, first][:].bitcast(F32),
            )

        def content_scores(n):
            i, a = n // TT, n % TT
            lhsT, rhs = qk_t[i][:, T + a * P : T + (a + 1) * P], qk_t[i][:, :T]
            if added_on_tensor(n):
                sum_ps = psum_sum.tile([P, T], F32, name="sum_ps", tag="sum")
                nc.tensor.matmul(sum_ps[:], lhsT=lhsT, rhs=rhs, start=True, stop=False)
                nc.tensor.matmul(
                    sum_ps[:], lhsT=ident_bf[:], rhs=bd_sb[i][:, a, :], start=False, stop=True
                )
                summed[n] = sum_ps[:]
            else:
                ac_ps[n] = psum_ac.tile([P, T], F32, name="ac_ps")
                nc.tensor.matmul(ac_ps[n][:], lhsT=lhsT, rhs=rhs, start=True, stop=True)

        def add_shifted(n):
            i, a = n // TT, n % TT
            if a == 0:
                score[i] = work.tile([P, TT, T], F32, name="score")
                row_max[i] = work.tile([P, TT], F32, name="row_max")
                neg_max[i] = work.tile([P, TT], F32, name="neg_max")
            if n not in summed:
                summed[n] = score[i][:, a, :]
                nc.vector.tensor_tensor(
                    out=summed[n], in0=ac_ps[n][:], in1=bd_sb[i][:, a, :], op=ALU.add
                )

        def maximum(n):
            i, a = n // TT, n % TT
            nc.vector.tensor_reduce(
                out=row_max[i][:, a : a + 1], in_=summed[n], axis=mybir.AxisListType.X,
                op=ALU.max,
            )
            nc.gpsimd.tensor_scalar(
                out=neg_max[i][:, a : a + 1], in0=row_max[i][:, a : a + 1], scalar1=-SCALE,
                scalar2=0.0, op0=ALU.mult, op1=ALU.add,
            )

        def exponentials(n):
            i, a = n // TT, n % TT
            if a == 0:
                e_sb[i] = work.tile([P, TT, T], BF16, name="e_sb")
                if i % GROUP == 0:
                    row_sum[i // GROUP] = work.tile([P, GROUP * TT], F32, name="row_sum", bufs=4)
            column = n % (GROUP * TT)
            nc.scalar.activation(
                out=e_sb[i][:, a, :], in_=summed[n], func=ACT.Exp,
                bias=neg_max[i][:, a : a + 1], scale=SCALE,
                accum_out=row_sum[i // GROUP][:, column : column + 1],
            )

        def transpose_e(n):
            i, a, m = n // TT, n % TT, n // 2
            if n % 2 == 0:
                e_ps[m] = psum_e.tile([P, 2, 2 * P], F32, name="e_ps")
            words = e_sb[i][:].bitcast(F32)
            for u in range(2):
                nc.tensor.transpose(
                    e_ps[m][:, u, (n % 2) * P : (n % 2 + 1) * P],
                    words[:, a, u * P : (u + 1) * P],
                    ident_f32[:],
                )

        def regroup_e(i, first, last):
            if first == 0:
                e_grouped[i] = work.tile([P, T * PACK], BF16, name="e_grouped", align_bytes=64)
            words = e_grouped[i][:].bitcast(F32).rearrange("p (t u) -> p t u", u=2)
            in_half = slice((first % 2) * P, (first % 2 + last - first) * P)
            nc.scalar.copy(
                out=words[:, first * P : last * P, :],
                in_=e_ps[2 * i + first // 2][:, :, in_half].rearrange("p u t -> p t u"),
            )

        def quantise_e(i, first, last):
            if first == 0:
                e_codes[i] = work.tile([P, T], U32, name="e_codes", bufs=6, align_bytes=64)
                e_scales[i] = work.tile([P, T], U8, name="e_scales", bufs=6, align_bytes=64)
            queries = slice(first * P, last * P)
            nc.vector.quantize_mx(
                out=e_codes[i][:, queries].bitcast(FP8X4),
                scales=e_scales[i][:, queries],
                in_=e_grouped[i][:, first * P * PACK : last * P * PACK],
            )

        def invert_sums(g):
            sums_inv = work.tile([P, GROUP * TT], F32, name="inv_sum", bufs=4)
            nc.vector.reciprocal(sums_inv[:], row_sum[g][:])
            for j in range(GROUP):
                inv_sum[g * GROUP + j] = sums_inv[:, j * TT : (j + 1) * TT]

        def attend(i):
            tag = "o" if i < N_HEADS - 1 else "v"
            o_ps[i] = psum_mx.tile([P, TT, HD], F32, name="o_ps", tag=tag)
            for a in range(TT):
                nc.tensor.matmul_mx(
                    out=o_ps[i][:, a, :],
                    lhsT=e_codes[i][:, a * P : (a + 1) * P].bitcast(FP8X4),
                    lhsT_scale=e_scales[i][:, a * P : (a + 1) * P],
                    rhs=v_codes[i][:].bitcast(FP8X4),
                    rhs_scale=v_scales[i][:],
                    start=True,
                    stop=True,
                )

        def normalise(i, a):
            if a == 0:
                o_sb[i] = work.tile([P, TT, HD], F32, name="o_sb", bufs=4)
            if i == N_HEADS - 1:
                nc.vector.tensor_scalar_mul(
                    out=o_sb[i][:, a, :], in0=o_ps[i][:, a, :], scalar1=inv_sum[i][:, a : a + 1]
                )
            else:
                nc.scalar.activation(
                    out=o_sb[i][:, a, :], in_=o_ps[i][:, a, :], func=ACT.Copy,
                    scale=inv_sum[i][:, a : a + 1],
                )

        def store_outputs(i, first, last):
            b, h = i // H, i % H
            nc.sync.dma_start(
                out=out[b].rearrange("(a p) e -> p a e", p=P)[:, first:last, h * HD : (h + 1) * HD],
                in_=o_sb[i][:, first:last],
            )

        request_group(0)
        request_head(0, 0, 2)
        request_x(0)
        request_head(0, 2, TT)
        request_head(1)
        request_group(1)
        for n in range(QK_LAG, attend_slot(N_HEADS - 1) + 3):
            i = unit(n, TT, N_HEADS)
            if i is not None:
                request_head(i + 2)
                if i % GROUP == 0:
                    request_group(i // GROUP + 2)
                if i == H // 2:
                    request_x(1)

            t = unit(n - EXP_LAG, 1, N_TILES)
            if t is not None:
                exponentials(t)

            t = unit(n + 1, 1, N_TILES)
            if t is not None and not added_on_tensor(t):
                content_scores(t)
            t = unit(n - E_T_LAG, 1, N_TILES)
            if t is not None:
                transpose_e(t)
            for i in range(N_HEADS):
                if n == attend_slot(i):
                    attend(i)
            for i in range(N_HEADS):
                for part in range(2):
                    if n == value_slot(i) + part:
                        project_values(i, part)

            t = unit(n, 1, N_TILES)
            if t is not None and added_on_tensor(t):
                content_scores(t)

            for i in range(N_HEADS):
                if n == value_slot(i) + 2:
                    add_bias(i)
            t = unit(n, 1, N_TILES)
            if t is not None:
                add_shifted(t)
            t = unit(n - 1, 1, N_TILES)
            if t is not None:
                maximum(t)
            m = unit(n - QUANT_LAG, 2, N_HALVES - 1)
            if m is not None:
                quantise_e(m // 2, 2 * (m % 2), 2 * (m % 2) + 2)
            t = n - LAST_TILE_LAG - 1
            if N_TILES - 2 <= t < N_TILES:
                quantise_e(N_HEADS - 1, t % TT, t % TT + 1)
            for i in range(N_HEADS):
                if n == value_slot(i) + 4:
                    quantise_v(i)
            for b in range(B):
                if n == X_START[b] + PACK:
                    quantise_x(b, 0, 2)
                if n == X_START[b] + 2 * PACK:
                    quantise_x(b, 2, PACK)
            h = unit(n - W_LAG - 2, TT, H)
            if h is not None:
                quantise_w(h)
            for i in range(N_HEADS):
                if i % GROUP == 0 and n == attend_slot(i) - 1:
                    invert_sums(i // GROUP)

            m = unit(n - REGROUP_LAG, 2, N_HALVES - 1)
            if m is not None:
                regroup_e(m // 2, 2 * (m % 2), 2 * (m % 2) + 2)
            t = n - LAST_TILE_LAG
            if N_TILES - 2 <= t < N_TILES:
                regroup_e(N_HEADS - 1, t % TT, t % TT + 1)
            i = unit(n - QK_LAG - 1, TT, N_HEADS)
            if i is not None:
                for first, last in qk_pieces(i):
                    copy_qk(i, first, last)
            h = unit(n - W_LAG - 1, TT, H)
            if h is not None:
                regroup_w(h)
            for b in range(B):
                r = unit(n - X_START[b] - 1, 2, PACK)
                if r is not None:
                    regroup_x(b, r)
            for i in range(N_HEADS):
                for half in range(2):
                    if n == attend_slot(i) + 1 + half:
                        normalise(i, 2 * half)
                        normalise(i, 2 * half + 1)
                        if i >= N_HEADS - 2:
                            store_outputs(i, 2 * half, 2 * half + 2)
                        elif half == 1:
                            store_outputs(i, 0, TT)

            i = unit(n - QK_LAG, TT, N_HEADS)
            if i is not None:
                for first, last in qk_pieces(i):
                    transpose_qk(i, first, last)
            h = unit(n - W_LAG, TT, H)
            if h is not None:
                transpose_w(h)
            for b in range(B):
                r = unit(n - X_START[b], 2, PACK)
                if r is not None:
                    transpose_x(b, r)
